import numpy as np
import ml_dtypes


def mxq(x, axis, fmt="e4m3"):
    dtype, down = {"e4m3": (ml_dtypes.float8_e4m3fn, 7), "e5m2": (ml_dtypes.float8_e5m2, 14)}[fmt]
    v = np.moveaxis(np.asarray(x, np.float32).astype(ml_dtypes.bfloat16).astype(np.float64), axis, -1)
    blocks = v.reshape(v.shape[:-1] + (-1, 32))
    amax = np.abs(blocks).max(-1, keepdims=True)
    byte = np.maximum(np.where(amax > 0, np.frexp(amax)[1] - 1 + 127, 0) - down, 1)
    scale = np.exp2(byte - 127.0)
    codes = (blocks / scale).astype(np.float32).astype(dtype).astype(np.float64)
    return np.moveaxis((codes * scale).reshape(v.shape), -1, axis)


WIDE = False


def mx_kscale(k):
    if not WIDE:
        return np.ones(k)
    levels = np.array([10, -10, 5, -5, 0])
    a = np.random.permutation(np.resize(levels, k // 512 * 4)).reshape(k // 512, 4)
    idx = np.arange(k)
    return np.exp2(a[idx // 512, idx % 128 // 32])


BF16 = ml_dtypes.bfloat16


def bf(x):
    return np.asarray(x, np.float32).astype(BF16)


def f64(x):
    return np.asarray(x).astype(np.float64)


E2M1 = np.array([0.0, 0.5, 1.0, 1.5, 2.0, 3.0, 4.0, 6.0, -0.0, -0.5, -1.0, -1.5, -2.0, -3.0, -4.0, -6.0])


def pack_weight(w, fmt):
    k, n = w.shape
    w = f64(bf(w)).reshape(k // 32, 32, n)
    amax = np.abs(w).max(1)
    if fmt == "e4m3":
        byte = np.frexp(amax)[1] - 1 + 127 - 7
    else:
        mant, ex = np.frexp(amax / 6.0)
        byte = np.where(mant > 0.5, ex, ex - 1) + 127
    byte = np.clip(np.where(amax > 0, byte, 1), 1, 254)
    scaled = (w * np.exp2(127.0 - byte)[:, None, :]).reshape(k, n).astype(np.float32)
    by_word = np.ascontiguousarray(scaled.reshape(k // 512, 128, 4, n).transpose(0, 1, 3, 2))
    if fmt == "e4m3":
        words = by_word.astype(ml_dtypes.float8_e4m3fn).view(np.uint8)
    else:
        c = by_word.astype(ml_dtypes.float4_e2m1fn).view(np.uint8) & 0xF
        words = c[..., 0::2] | (c[..., 1::2] << 4)
    return np.ascontiguousarray(words), np.ascontiguousarray(byte.astype(np.uint8).reshape(k // 512, 16, n))


def unpack_weight(words, scales, fmt):
    g, p, n, _ = words.shape
    if fmt == "e4m3":
        vals = np.ascontiguousarray(words).view(ml_dtypes.float8_e4m3fn).astype(np.float64)
    else:
        nib = np.empty((g, p, n, 4), np.uint8)
        nib[..., 0::2] = words & 0xF
        nib[..., 1::2] = words >> 4
        vals = E2M1[nib]
    vals = vals * np.repeat(np.exp2(scales.astype(np.float64) - 127.0), 8, axis=1)[..., None]
    return vals.transpose(0, 1, 3, 2).reshape(g * 512, n)


N, K, F, NB = 4096, 512, 128, 32
EPS = 1e-6
FMT = "e4m3"


def erf(v):
    a = np.minimum(np.abs(v), 6.0)
    term = a.copy()
    total = a.copy()
    for n in range(1, 130):
        term = term * (2.0 * a * a / (2.0 * n + 1.0))
        total = total + term
    return np.sign(v) * (2.0 / np.sqrt(np.pi)) * np.exp(-a * a) * total


def gelu(v):
    return 0.5 * v * (1.0 + erf(v / np.sqrt(2.0)))


def setup_inputs():
    s = mx_kscale(K)
    edge = np.random.random_sample((N, N)) < NB / N
    x = bf(np.random.standard_normal((N, K)) * s)
    adj = bf(np.random.random_sample((N, N)) * edge)
    W1_words, W1_scales = pack_weight(np.random.standard_normal((K, F)) * 3.0 / np.sqrt(K) / s[:, None], FMT)
    return {"x": x,
            "adj": adj,
            "W1_words": W1_words,
            "W1_scales": W1_scales,
            "b1": bf(np.random.standard_normal(F) * 0.3),
            "ln_gamma": bf(1.0 + 0.1 * np.random.standard_normal(F)),
            "ln_beta": bf(0.1 * np.random.standard_normal(F))}


def reference(x, adj, W1_words, W1_scales, b1, ln_gamma, ln_beta):
    a = f64(adj)
    h = (mxq(f64(x), 1, "e4m3") @ unpack_weight(W1_words, W1_scales, FMT)) + f64(b1)
    deg = a.sum(axis=1) + 1.0
    dinv = np.where(deg > 0, deg ** -0.5, 0.0)
    hs = dinv[:, None] * h
    agg = (mxq(a, 1, "e4m3") @ mxq(hs, 0, "e4m3")) + hs
    g = gelu(dinv[:, None] * agg)
    mu = g.mean(axis=-1, keepdims=True)
    var = ((g - mu) ** 2).mean(axis=-1, keepdims=True)
    return (g - mu) / np.sqrt(var + EPS) * f64(ln_gamma) + f64(ln_beta)

@@ -1,0 +1,320 @@
+from contextlib import ExitStack
+
+import concourse.mybir as mybir
+from concourse.masks import make_identity
+
+F32 = mybir.dt.float32
+BF16 = mybir.dt.bfloat16
+U32 = mybir.dt.uint32
+U8 = mybir.dt.uint8
+I32 = mybir.dt.int32
+FP8X4 = mybir.dt.float8_e4m3fn_x4
+ACT = mybir.ActivationFunctionType
+ALU = mybir.AluOpType
+AXIS_X = mybir.AxisListType.X
+
+P = 128
+NODES = 4096
+K_IN = 512
+FEAT = 128
+EPS = 1e-6
+PACK = 4
+K_PASS = P * PACK
+PASSES = NODES // K_PASS
+TILES = NODES // P
+QUAD = K_PASS // P
+QUADS = TILES // QUAD
+AHEAD = 3
+
+FLOPS = 2 * NODES * K_IN * FEAT + 2 * NODES * NODES * FEAT
+
+
+def tile_gcnlayer_pa_t_kernel(tc, x, adj, W1_words, W1_scales, b1, ln_gamma, ln_beta, out):
+    nc = tc.nc
+
+    x_view = x.rearrange("(g u p e) k -> g p u (e k)", u=2, p=P, e=2)
+    adj_view = adj.rearrange("(c p e) j -> c e p j", p=P, e=2)
+    out_view = out.rearrange("(g u p e) f -> g p u (e f)", u=2, p=P, e=2)
+
+    with ExitStack() as ctx:
+        const = ctx.enter_context(tc.tile_pool(name="const", bufs=1))
+        keep = ctx.enter_context(tc.tile_pool(name="keep", bufs=1))
+        stream = ctx.enter_context(tc.tile_pool(name="stream", bufs=2))
+        flip_psum = ctx.enter_context(tc.psum_pool(name="flip_psum", bufs=4))
+        sum_psum = ctx.enter_context(tc.psum_pool(name="sum_psum", bufs=2))
+        deg_psum = ctx.enter_context(tc.psum_pool(name="deg_psum", bufs=2))
+        ctx.enter_context(tc.manual_schedule())
+
+        def load_x(quad):
+            x_sb = stream.tile([P, 2, 2 * K_IN], BF16, name="x_sb")
+            nc.sync.dma_start(out=x_sb[:], in_=x_view[quad])
+            return x_sb
+
+        def load_adj(tile_no):
+            adj_sb = stream.tile([P, NODES], BF16, name="adj_sb", bufs=AHEAD + 1)
+            nc.sync.dma_start(out=adj_sb[:], in_=adj_view[tile_no // 2, tile_no % 2])
+            return adj_sb
+
+        x_of = {0: load_x(0)}
+        w1_codes = const.tile([P, FEAT], U32, align_bytes=64)
+        nc.sync.dma_start(
+            out=w1_codes[:].bitcast(I32),
+            in_=W1_words[0].rearrange("p n t -> p (n t)").bitcast(I32),
+        )
+        w1_planes = const.tile([P, FEAT], U8, align_bytes=64)
+        nc.vector.memset(w1_planes[:].bitcast(I32), 0)
+        for quadrant in range(4):
+            nc.sync.dma_start(
+                out=w1_planes[32 * quadrant : 32 * quadrant + 4, :].bitcast(I32),
+                in_=W1_scales[0, 4 * quadrant : 4 * quadrant + 4, :].bitcast(I32),
+            )
+        adj_of = {}
+        for tile_no in range(AHEAD):
+            adj_of[tile_no] = load_adj(tile_no)
+
+        rows_bf = const.tile([P, 3, FEAT], BF16)
+        for i, vector in enumerate((b1, ln_gamma, ln_beta)):
+            nc.scalar.dma_start(out=rows_bf[:, i, :], in_=vector.partition_broadcast(P))
+        warm = const.tile([P, 1], F32)
+        nc.vector.memset(warm[:], 0.0)
+        nc.scalar.activation(out=warm[:], in_=warm[:], func=ACT.Gelu)
+
+        ident = const.tile([P, P], F32)
+        make_identity(nc, ident[:])
+        ones = const.tile([P, 2], BF16)
+        nc.vector.memset(ones[:], 1.0)
+        neg_half = const.tile([P, QUAD], F32)
+        nc.vector.memset(neg_half[:], -0.5)
+        fold = const.tile([P, PACK, P], F32)
+        nc.vector.memset(fold[:], 0.0)
+        four_to_one = const.tile([P, P // PACK], F32)
+        nc.vector.tensor_reduce(
+            out=four_to_one[:], in_=ident[:].rearrange("p (i t) -> p i t", t=PACK), axis=AXIS_X, op=ALU.add
+        )
+        for s in range(PACK):
+            nc.vector.tensor_copy(out=fold[:, s, 32 * s : 32 * s + 32], in_=four_to_one[:])
+        rows = const.tile([P, 3, FEAT], F32)
+        b1_row, gamma_row, beta_row = rows[:, 0, :], rows[:, 1, :], rows[:, 2, :]
+
+        codes = keep.tile([P, TILES, PASSES, P], U32, align_bytes=64)
+        planes = keep.tile([P, QUADS, PASSES, P], U8, align_bytes=64)
+        hs_codes = keep.tile([P, PASSES, FEAT], U32, align_bytes=64)
+        hs_planes = keep.tile([P, PASSES, FEAT], U8, align_bytes=64)
+        acc = keep.tile([P, TILES, FEAT], F32)
+        dinv = keep.tile([P, TILES], F32)
+        g_sum = keep.tile([P, TILES], F32)
+        neg_mean = keep.tile([P, TILES], F32)
+        sq_sum = keep.tile([P, TILES], F32)
+        var_eps = keep.tile([P, TILES], F32)
+        rstd = keep.tile([P, TILES], F32)
+
+        def tiles_of(quad):
+            return slice(QUAD * quad, QUAD * (quad + 1))
+
+        def flip_and_quantise(words, codes_out, planes_out):
+            bank = flip_psum.tile([P, 2, 2, P], F32, name="bank")
+            for a in range(2):
+                for v in range(2):
+                    nc.tensor.transpose(bank[:, a, v, :], words[a][v], ident[:])
+            grouped = stream.tile([P, 2, P, PACK], BF16, name="grouped", bufs=7, align_bytes=64)
+            nc.scalar.copy(out=grouped[:].bitcast(F32), in_=bank[:].rearrange("p a v i -> p a i v"))
+            nc.vector.quantize_mx(
+                out=codes_out.bitcast(FP8X4),
+                scales=planes_out,
+                in_=grouped[:].rearrange("p a i t -> p (a i t)"),
+            )
+            return grouped
+
+        def flip_x(quad):
+            x_words = x_of[quad][:].bitcast(F32)
+            quantised = []
+            for u in range(2):
+                x_codes = stream.tile([P, 2, P], U32, name="x_codes", align_bytes=64)
+                x_planes = stream.tile([P, 2, P], U8, name="x_planes", align_bytes=64)
+                flip_and_quantise(
+                    [[x_words[:, u, 256 * e + v : 256 * (e + 1) : 2] for v in range(2)] for e in range(2)],
+                    x_codes[:].rearrange("p a i -> p (a i)"),
+                    x_planes[:].rearrange("p a i -> p (a i)"),
+                )
+                quantised.append((x_codes, x_planes))
+            return quantised
+
+        def hidden(quad, quantised):
+            sums = sum_psum.tile([P, QUAD, FEAT], F32, name="sums")
+            for u in range(2):
+                x_codes, x_planes = quantised[u]
+                for e in range(2):
+                    nc.tensor.matmul_mx(
+                        out=sums[:, 2 * u + e, :],
+                        lhsT=x_codes[:, e, :].bitcast(FP8X4),
+                        lhsT_scale=x_planes[:, e, :],
+                        rhs=w1_codes[:].bitcast(FP8X4),
+                        rhs_scale=w1_planes[:],
+                        start=True,
+                        stop=True,
+                    )
+            nc.vector.tensor_tensor(
+                out=acc[:, tiles_of(quad), :],
+                in0=sums[:],
+                in1=b1_row.unsqueeze(1).to_broadcast([P, QUAD, FEAT]),
+                op=ALU.add,
+            )
+
+        def flip_adj(tile_no, k):
+            adj_words = adj_of[tile_no][:].bitcast(F32)
+            return flip_and_quantise(
+                [[adj_words[:, 256 * (k + a) + P * u : 256 * (k + a) + P * (u + 1)] for u in range(2)]
+                 for a in range(2)],
+                codes[:, tile_no, k : k + 2, :].rearrange("p a i -> p (a i)"),
+                planes[4 * (tile_no % QUAD) : P, tile_no // QUAD, k : k + 2, :].rearrange("p a i -> p (a i)"),
+            )
+
+        def row_sums(part, r, k, grouped):
+            for a in range(2):
+                for s in range(PACK):
+                    nc.tensor.matmul(
+                        out=part[:, s, r, k + a, :],
+                        lhsT=grouped[:, a, 32 * s : 32 * (s + 1), :].rearrange("p i t -> p (i t)"),
+                        rhs=ones[:],
+                        start=True,
+                        stop=True,
+                    )
+
+        def gather(part):
+            part_sb = stream.tile([P, PACK, QUAD * PASSES], F32, name="part_sb")
+            nc.vector.tensor_copy(
+                out=part_sb[:], in_=part[:, :, :, :, 0].rearrange("p s r k -> p s (r k)")
+            )
+            return part_sb
+
+        def degrees(quad, part_sb):
+            sums = sum_psum.tile([P, QUAD, FEAT], F32, name="sums")
+            by_pass = sums[:, 0, 0 : QUAD * PASSES]
+            for s in range(PACK):
+                nc.tensor.matmul(
+                    out=by_pass, lhsT=fold[:, s, :], rhs=part_sb[:, s, :],
+                    start=(s == 0), stop=(s == PACK - 1),
+                )
+            row_sum = stream.tile([P, QUAD], F32, name="row_sum")
+            nc.vector.tensor_reduce(
+                out=row_sum[:], in_=by_pass.rearrange("p (r k) -> p r k", k=PASSES), axis=AXIS_X, op=ALU.add
+            )
+            deg = stream.tile([P, QUAD], F32, name="deg")
+            nc.gpsimd.tensor_scalar(
+                out=deg[:], in0=row_sum[:], scalar1=1.0, scalar2=1.0, op0=ALU.mult, op1=ALU.add
+            )
+            nc.gpsimd.tensor_tensor(out=dinv[:, tiles_of(quad)], in0=deg[:], in1=neg_half[:], op=ALU.pow)
+
+        def scale(quad):
+            mine = tiles_of(quad)
+            hs_grouped = stream.tile([P, FEAT, PACK], BF16, name="hs_grouped", align_bytes=64)
+            nc.vector.tensor_tensor(
+                out=hs_grouped[:],
+                in0=acc[:, mine, :].rearrange("p t f -> p f t"),
+                in1=dinv[:, mine].unsqueeze(1).to_broadcast([P, FEAT, PACK]),
+                op=ALU.mult,
+            )
+            nc.vector.quantize_mx(
+                out=hs_codes[:, quad, :].bitcast(FP8X4),
+                scales=hs_planes[:, quad, :],
+                in_=hs_grouped[:].rearrange("p f t -> p (f t)"),
+            )
+            nc.gpsimd.tensor_tensor(
+                out=acc[:, mine, :],
+                in0=acc[:, mine, :],
+                in1=dinv[:, mine].unsqueeze(2).to_broadcast([P, QUAD, FEAT]),
+                op=ALU.mult,
+            )
+
+        grouped_of = {}
+        part_of = {}
+        part_sb_of = {}
+        x_quantised = {}
+        for step in range(TILES + 3):
+            quad, r = divmod(step, QUAD)
+            if step < TILES and r == 0:
+                x_quantised[quad] = flip_x(quad)
+            if step + AHEAD < TILES:
+                adj_of[step + AHEAD] = load_adj(step + AHEAD)
+            if r == 1 and quad + 1 < QUADS:
+                x_of[quad + 1] = load_x(quad + 1)
+            for k in range(0, PASSES, 2):
+                if 1 <= step <= TILES:
+                    before = step - 1
+                    if before % QUAD == 0 and k == 0:
+                        part_of[before // QUAD] = deg_psum.tile([P, PACK, QUAD, PASSES, 2], F32, name="part")
+                    row_sums(part_of[before // QUAD], before % QUAD, k, grouped_of[before, k])
+                if step < TILES:
+                    grouped_of[step, k] = flip_adj(step, k)
+            if step < TILES and r == 1:
+                if quad == 0:
+                    nc.vector.tensor_copy(out=rows[:], in_=rows_bf[:])
+                hidden(quad, x_quantised[quad])
+            if quad >= 1 and r == 0:
+                part_sb_of[quad - 1] = gather(part_of[quad - 1])
+            if quad >= 1 and r == 1:
+                degrees(quad - 1, part_sb_of[quad - 1])
+            if quad >= 1 and r == 2:
+                scale(quad - 1)
+
+        def aggregate(quad):
+            sums = sum_psum.tile([P, QUAD, FEAT], F32, name="sums")
+            for r in range(QUAD):
+                for g in range(PASSES):
+                    nc.tensor.matmul_mx(
+                        out=sums[:, r, :],
+                        lhsT=codes[:, QUAD * quad + r, g, :].bitcast(FP8X4),
+                        lhsT_scale=planes[4 * r : P, quad, g, :],
+                        rhs=hs_codes[:, g, :].bitcast(FP8X4),
+                        rhs_scale=hs_planes[:, g, :],
+                        start=(g == 0),
+                        stop=(g == PASSES - 1),
+                    )
+            mine = tiles_of(quad)
+            nc.vector.tensor_tensor(out=acc[:, mine, :], in0=sums[:], in1=acc[:, mine, :], op=ALU.add)
+            for t in range(QUAD * quad, QUAD * (quad + 1)):
+                nc.scalar.activation(
+                    out=acc[:, t, :], in_=acc[:, t, :], func=ACT.Gelu,
+                    scale=dinv[:, t : t + 1], accum_out=g_sum[:, t : t + 1],
+                )
+            nc.gpsimd.tensor_scalar(
+                out=neg_mean[:, mine], in0=g_sum[:, mine], scalar1=-1.0 / FEAT, scalar2=0.0,
+                op0=ALU.mult, op1=ALU.add,
+            )
+
+        def spread(quad):
+            mine = tiles_of(quad)
+            for t in range(QUAD * quad, QUAD * (quad + 1)):
+                squares = stream.tile([P, FEAT], F32, name="squares")
+                nc.scalar.activation(
+                    out=squares[:], in_=acc[:, t, :], func=ACT.Square,
+                    bias=neg_mean[:, t : t + 1], accum_out=sq_sum[:, t : t + 1],
+                )
+            nc.gpsimd.tensor_scalar(
+                out=var_eps[:, mine], in0=sq_sum[:, mine], scalar1=1.0 / FEAT, scalar2=EPS,
+                op0=ALU.mult, op1=ALU.add,
+            )
+            nc.gpsimd.tensor_tensor(out=rstd[:, mine], in0=var_eps[:, mine], in1=neg_half[:], op=ALU.pow)
+
+        def normalise_and_store(quad):
+            for t in range(QUAD * quad, QUAD * (quad + 1)):
+                nc.vector.scalar_tensor_tensor(
+                    out=acc[:, t, :], in0=acc[:, t, :], scalar=neg_mean[:, t : t + 1], in1=gamma_row,
+                    op0=ALU.add, op1=ALU.mult,
+                )
+                nc.vector.scalar_tensor_tensor(
+                    out=acc[:, t, :], in0=acc[:, t, :], scalar=rstd[:, t : t + 1], in1=beta_row,
+                    op0=ALU.mult, op1=ALU.add,
+                )
+            nc.sync.dma_start(
+                out=out_view[quad],
+                in_=acc[:, tiles_of(quad), :].rearrange("p (u e) f -> p u (e f)", u=2),
+            )
+
+        for quad in range(QUADS + 2):
+            if quad < QUADS:
+                aggregate(quad)
+            if 1 <= quad <= QUADS:
+                spread(quad - 1)
+            if quad >= 2:
+                normalise_and_store(quad - 2)

@@ -25,6 +25,9 @@ TILES = NODES // P
 QUAD = K_PASS // P
 QUADS = TILES // QUAD
 AHEAD = 3
+X_AHEAD = 2
+EARLY = 2
+ONES = 14
 
 FLOPS = 2 * NODES * K_IN * FEAT + 2 * NODES * NODES * FEAT
 
@@ -55,7 +58,9 @@ def tile_gcnlayer_pa_t_kernel(tc, x, adj, W1_words, W1_scales, b1, ln_gamma, ln_
             nc.sync.dma_start(out=adj_sb[:], in_=adj_view[tile_no // 2, tile_no % 2])
             return adj_sb
 
-        x_of = {0: load_x(0)}
+        x_of = {}
+        for quad in range(X_AHEAD):
+            x_of[quad] = load_x(quad)
         w1_codes = const.tile([P, FEAT], U32, align_bytes=64)
         nc.sync.dma_start(
             out=w1_codes[:].bitcast(I32),
@@ -81,7 +86,7 @@ def tile_gcnlayer_pa_t_kernel(tc, x, adj, W1_words, W1_scales, b1, ln_gamma, ln_
 
         ident = const.tile([P, P], F32)
         make_identity(nc, ident[:])
-        ones = const.tile([P, 2], BF16)
+        ones = const.tile([P, ONES], BF16)
         nc.vector.memset(ones[:], 1.0)
         neg_half = const.tile([P, QUAD], F32)
         nc.vector.memset(neg_half[:], -0.5)
@@ -116,7 +121,7 @@ def tile_gcnlayer_pa_t_kernel(tc, x, adj, W1_words, W1_scales, b1, ln_gamma, ln_
             for a in range(2):
                 for v in range(2):
                     nc.tensor.transpose(bank[:, a, v, :], words[a][v], ident[:])
-            grouped = stream.tile([P, 2, P, PACK], BF16, name="grouped", bufs=7, align_bytes=64)
+            grouped = stream.tile([P, 2, P, PACK], BF16, name="grouped", bufs=10, align_bytes=64)
             nc.scalar.copy(out=grouped[:].bitcast(F32), in_=bank[:].rearrange("p a v i -> p a i v"))
             nc.vector.quantize_mx(
                 out=codes_out.bitcast(FP8X4),
@@ -129,8 +134,8 @@ def tile_gcnlayer_pa_t_kernel(tc, x, adj, W1_words, W1_scales, b1, ln_gamma, ln_
             x_words = x_of[quad][:].bitcast(F32)
             quantised = []
             for u in range(2):
-                x_codes = stream.tile([P, 2, P], U32, name="x_codes", align_bytes=64)
-                x_planes = stream.tile([P, 2, P], U8, name="x_planes", align_bytes=64)
+                x_codes = stream.tile([P, 2, P], U32, name="x_codes", bufs=2 * X_AHEAD, align_bytes=64)
+                x_planes = stream.tile([P, 2, P], U8, name="x_planes", bufs=2 * X_AHEAD, align_bytes=64)
                 flip_and_quantise(
                     [[x_words[:, u, 256 * e + v : 256 * (e + 1) : 2] for v in range(2)] for e in range(2)],
                     x_codes[:].rearrange("p a i -> p (a i)"),
@@ -169,39 +174,32 @@ def tile_gcnlayer_pa_t_kernel(tc, x, adj, W1_words, W1_scales, b1, ln_gamma, ln_
                 planes[4 * (tile_no % QUAD) : P, tile_no // QUAD, k : k + 2, :].rearrange("p a i -> p (a i)"),
             )
 
-        def row_sums(part, r, k, grouped):
-            for a in range(2):
-                for s in range(PACK):
-                    nc.tensor.matmul(
-                        out=part[:, s, r, k + a, :],
-                        lhsT=grouped[:, a, 32 * s : 32 * (s + 1), :].rearrange("p i t -> p (i t)"),
-                        rhs=ones[:],
-                        start=True,
-                        stop=True,
-                    )
+        def row_sums(part, r, s, grouped):
+            for k in range(PASSES):
+                nc.tensor.matmul(
+                    out=part[:, r, s, :],
+                    lhsT=grouped[k // 2][:, k % 2, 32 * s : 32 * (s + 1), :].rearrange("p i t -> p (i t)"),
+                    rhs=ones[:],
+                    start=(k == 0),
+                    stop=(k == PASSES - 1),
+                )
 
         def gather(part):
-            part_sb = stream.tile([P, PACK, QUAD * PASSES], F32, name="part_sb")
-            nc.vector.tensor_copy(
-                out=part_sb[:], in_=part[:, :, :, :, 0].rearrange("p s r k -> p s (r k)")
-            )
+            part_sb = stream.tile([P, PACK, QUAD], F32, name="part_sb")
+            nc.vector.tensor_copy(out=part_sb[:], in_=part[:, :, :, 0].rearrange("p r s -> p s r"))
             return part_sb
 
         def degrees(quad, part_sb):
             sums = sum_psum.tile([P, QUAD, FEAT], F32, name="sums")
-            by_pass = sums[:, 0, 0 : QUAD * PASSES]
+            row_sum = sums[:, 0, 0:QUAD]
             for s in range(PACK):
                 nc.tensor.matmul(
-                    out=by_pass, lhsT=fold[:, s, :], rhs=part_sb[:, s, :],
+                    out=row_sum, lhsT=fold[:, s, :], rhs=part_sb[:, s, :],
                     start=(s == 0), stop=(s == PACK - 1),
                 )
-            row_sum = stream.tile([P, QUAD], F32, name="row_sum")
-            nc.vector.tensor_reduce(
-                out=row_sum[:], in_=by_pass.rearrange("p (r k) -> p r k", k=PASSES), axis=AXIS_X, op=ALU.add
-            )
             deg = stream.tile([P, QUAD], F32, name="deg")
-            nc.gpsimd.tensor_scalar(
-                out=deg[:], in0=row_sum[:], scalar1=1.0, scalar2=1.0, op0=ALU.mult, op1=ALU.add
+            nc.vector.tensor_scalar(
+                out=deg[:], in0=row_sum, scalar1=1.0, scalar2=0.0, op0=ALU.add, op1=ALU.add
             )
             nc.gpsimd.tensor_tensor(out=dinv[:, tiles_of(quad)], in0=deg[:], in1=neg_half[:], op=ALU.pow)
 
@@ -226,52 +224,69 @@ def tile_gcnlayer_pa_t_kernel(tc, x, adj, W1_words, W1_scales, b1, ln_gamma, ln_
                 op=ALU.mult,
             )
 
-        grouped_of = {}
-        part_of = {}
-        part_sb_of = {}
-        x_quantised = {}
-        for step in range(TILES + 3):
-            quad, r = divmod(step, QUAD)
-            if step < TILES and r == 0:
-                x_quantised[quad] = flip_x(quad)
-            if step + AHEAD < TILES:
-                adj_of[step + AHEAD] = load_adj(step + AHEAD)
-            if r == 1 and quad + 1 < QUADS:
-                x_of[quad + 1] = load_x(quad + 1)
-            for k in range(0, PASSES, 2):
-                if 1 <= step <= TILES:
-                    before = step - 1
-                    if before % QUAD == 0 and k == 0:
-                        part_of[before // QUAD] = deg_psum.tile([P, PACK, QUAD, PASSES, 2], F32, name="part")
-                    row_sums(part_of[before // QUAD], before % QUAD, k, grouped_of[before, k])
-                if step < TILES:
-                    grouped_of[step, k] = flip_adj(step, k)
-            if step < TILES and r == 1:
-                if quad == 0:
-                    nc.vector.tensor_copy(out=rows[:], in_=rows_bf[:])
-                hidden(quad, x_quantised[quad])
-            if quad >= 1 and r == 0:
-                part_sb_of[quad - 1] = gather(part_of[quad - 1])
-            if quad >= 1 and r == 1:
-                degrees(quad - 1, part_sb_of[quad - 1])
-            if quad >= 1 and r == 2:
-                scale(quad - 1)
-
-        def aggregate(quad):
+        def add_passes(quad, first, last):
             sums = sum_psum.tile([P, QUAD, FEAT], F32, name="sums")
             for r in range(QUAD):
-                for g in range(PASSES):
+                for g in range(first, last):
                     nc.tensor.matmul_mx(
                         out=sums[:, r, :],
                         lhsT=codes[:, QUAD * quad + r, g, :].bitcast(FP8X4),
                         lhsT_scale=planes[4 * r : P, quad, g, :],
                         rhs=hs_codes[:, g, :].bitcast(FP8X4),
                         rhs_scale=hs_planes[:, g, :],
-                        start=(g == 0),
-                        stop=(g == PASSES - 1),
+                        start=(g == first),
+                        stop=(g == last - 1),
                     )
             mine = tiles_of(quad)
             nc.vector.tensor_tensor(out=acc[:, mine, :], in0=sums[:], in1=acc[:, mine, :], op=ALU.add)
+
+        def gets_early_passes(quad):
+            return EARLY <= quad < QUADS - 1
+
+        nc.vector.tensor_copy(out=rows[:], in_=rows_bf[:])
+        x_quantised = {}
+        for quad in range(X_AHEAD):
+            x_quantised[quad] = flip_x(quad)
+        for quad in range(X_AHEAD):
+            hidden(quad, x_quantised[quad])
+
+        grouped_of = {}
+        part_of = {}
+        part_sb_of = {}
+        for step in range(TILES + 3):
+            quad, r = divmod(step, QUAD)
+            done = quad - 1
+            soon = quad + X_AHEAD
+            if r == 0 and soon < QUADS:
+                x_of[soon] = load_x(soon)
+            if step + AHEAD < TILES:
+                adj_of[step + AHEAD] = load_adj(step + AHEAD)
+            if r == 2 and soon < QUADS:
+                x_quantised[soon] = flip_x(soon)
+            for s in range(PACK):
+                if 1 <= step <= TILES:
+                    before = step - 1
+                    if before % QUAD == 0 and s == 0:
+                        part_of[before // QUAD] = deg_psum.tile([P, QUAD, PACK, ONES], F32, name="part")
+                    row_sums(part_of[before // QUAD], before % QUAD, s, grouped_of[before])
+                if step < TILES:
+                    if s == 0:
+                        grouped_of[step] = []
+                    grouped_of[step].append(flip_adj(step, 2 * s))
+            if done >= 0 and r == 0:
+                part_sb_of[done] = gather(part_of[done])
+            if done >= 0 and r == 1:
+                degrees(done, part_sb_of[done])
+            if done >= 0 and r == 2:
+                scale(done)
+            if r == 3 and soon < QUADS:
+                hidden(soon, x_quantised[soon])
+            if r == 3 and gets_early_passes(done):
+                add_passes(done, 0, EARLY)
+
+        def aggregate(quad):
+            add_passes(quad, EARLY if gets_early_passes(quad) else 0, PASSES)
+            mine = tiles_of(quad)
             for t in range(QUAD * quad, QUAD * (quad + 1)):
                 nc.scalar.activation(
                     out=acc[:, t, :], in_=acc[:, t, :], func=ACT.Gelu,

@@ -11,7 +11,6 @@ I32 = mybir.dt.int32
 FP8X4 = mybir.dt.float8_e4m3fn_x4
 ACT = mybir.ActivationFunctionType
 ALU = mybir.AluOpType
-AXIS_X = mybir.AxisListType.X
 
 P = 128
 NODES = 4096
@@ -25,9 +24,8 @@ TILES = NODES // P
 QUAD = K_PASS // P
 QUADS = TILES // QUAD
 AHEAD = 3
-X_AHEAD = 2
-EARLY = 2
-ONES = 14
+S_COLS = 1024
+V_HALF = (NODES - S_COLS) // 2
 
 FLOPS = 2 * NODES * K_IN * FEAT + 2 * NODES * NODES * FEAT
 
@@ -43,9 +41,8 @@ def tile_gcnlayer_pa_t_kernel(tc, x, adj, W1_words, W1_scales, b1, ln_gamma, ln_
         const = ctx.enter_context(tc.tile_pool(name="const", bufs=1))
         keep = ctx.enter_context(tc.tile_pool(name="keep", bufs=1))
         stream = ctx.enter_context(tc.tile_pool(name="stream", bufs=2))
-        flip_psum = ctx.enter_context(tc.psum_pool(name="flip_psum", bufs=4))
+        flip_psum = ctx.enter_context(tc.psum_pool(name="flip_psum", bufs=6))
         sum_psum = ctx.enter_context(tc.psum_pool(name="sum_psum", bufs=2))
-        deg_psum = ctx.enter_context(tc.psum_pool(name="deg_psum", bufs=2))
         ctx.enter_context(tc.manual_schedule())
 
         def load_x(quad):
@@ -58,9 +55,7 @@ def tile_gcnlayer_pa_t_kernel(tc, x, adj, W1_words, W1_scales, b1, ln_gamma, ln_
             nc.sync.dma_start(out=adj_sb[:], in_=adj_view[tile_no // 2, tile_no % 2])
             return adj_sb
 
-        x_of = {}
-        for quad in range(X_AHEAD):
-            x_of[quad] = load_x(quad)
+        x_of = {0: load_x(0)}
         w1_codes = const.tile([P, FEAT], U32, align_bytes=64)
         nc.sync.dma_start(
             out=w1_codes[:].bitcast(I32),
@@ -86,18 +81,8 @@ def tile_gcnlayer_pa_t_kernel(tc, x, adj, W1_words, W1_scales, b1, ln_gamma, ln_
 
         ident = const.tile([P, P], F32)
         make_identity(nc, ident[:])
-        ones = const.tile([P, ONES], BF16)
-        nc.vector.memset(ones[:], 1.0)
         neg_half = const.tile([P, QUAD], F32)
         nc.vector.memset(neg_half[:], -0.5)
-        fold = const.tile([P, PACK, P], F32)
-        nc.vector.memset(fold[:], 0.0)
-        four_to_one = const.tile([P, P // PACK], F32)
-        nc.vector.tensor_reduce(
-            out=four_to_one[:], in_=ident[:].rearrange("p (i t) -> p i t", t=PACK), axis=AXIS_X, op=ALU.add
-        )
-        for s in range(PACK):
-            nc.vector.tensor_copy(out=fold[:, s, 32 * s : 32 * s + 32], in_=four_to_one[:])
         rows = const.tile([P, 3, FEAT], F32)
         b1_row, gamma_row, beta_row = rows[:, 0, :], rows[:, 1, :], rows[:, 2, :]
 
@@ -106,6 +91,8 @@ def tile_gcnlayer_pa_t_kernel(tc, x, adj, W1_words, W1_scales, b1, ln_gamma, ln_
         hs_codes = keep.tile([P, PASSES, FEAT], U32, align_bytes=64)
         hs_planes = keep.tile([P, PASSES, FEAT], U8, align_bytes=64)
         acc = keep.tile([P, TILES, FEAT], F32)
+        sum_s = keep.tile([P, TILES], F32)
+        sum_v = keep.tile([P, TILES], F32)
         dinv = keep.tile([P, TILES], F32)
         g_sum = keep.tile([P, TILES], F32)
         neg_mean = keep.tile([P, TILES], F32)
@@ -121,7 +108,7 @@ def tile_gcnlayer_pa_t_kernel(tc, x, adj, W1_words, W1_scales, b1, ln_gamma, ln_
             for a in range(2):
                 for v in range(2):
                     nc.tensor.transpose(bank[:, a, v, :], words[a][v], ident[:])
-            grouped = stream.tile([P, 2, P, PACK], BF16, name="grouped", bufs=10, align_bytes=64)
+            grouped = stream.tile([P, 2, P, PACK], BF16, name="grouped", bufs=6, align_bytes=64)
             nc.scalar.copy(out=grouped[:].bitcast(F32), in_=bank[:].rearrange("p a v i -> p a i v"))
             nc.vector.quantize_mx(
                 out=codes_out.bitcast(FP8X4),
@@ -134,8 +121,8 @@ def tile_gcnlayer_pa_t_kernel(tc, x, adj, W1_words, W1_scales, b1, ln_gamma, ln_
             x_words = x_of[quad][:].bitcast(F32)
             quantised = []
             for u in range(2):
-                x_codes = stream.tile([P, 2, P], U32, name="x_codes", bufs=2 * X_AHEAD, align_bytes=64)
-                x_planes = stream.tile([P, 2, P], U8, name="x_planes", bufs=2 * X_AHEAD, align_bytes=64)
+                x_codes = stream.tile([P, 2, P], U32, name="x_codes", align_bytes=64)
+                x_planes = stream.tile([P, 2, P], U8, name="x_planes", align_bytes=64)
                 flip_and_quantise(
                     [[x_words[:, u, 256 * e + v : 256 * (e + 1) : 2] for v in range(2)] for e in range(2)],
                     x_codes[:].rearrange("p a i -> p (a i)"),
@@ -174,34 +161,29 @@ def tile_gcnlayer_pa_t_kernel(tc, x, adj, W1_words, W1_scales, b1, ln_gamma, ln_
                 planes[4 * (tile_no % QUAD) : P, tile_no // QUAD, k : k + 2, :].rearrange("p a i -> p (a i)"),
             )
 
-        def row_sums(part, r, s, grouped):
-            for k in range(PASSES):
-                nc.tensor.matmul(
-                    out=part[:, r, s, :],
-                    lhsT=grouped[k // 2][:, k % 2, 32 * s : 32 * (s + 1), :].rearrange("p i t -> p (i t)"),
-                    rhs=ones[:],
-                    start=(k == 0),
-                    stop=(k == PASSES - 1),
-                )
-
-        def gather(part):
-            part_sb = stream.tile([P, PACK, QUAD], F32, name="part_sb")
-            nc.vector.tensor_copy(out=part_sb[:], in_=part[:, :, :, 0].rearrange("p r s -> p s r"))
-            return part_sb
-
-        def degrees(quad, part_sb):
-            sums = sum_psum.tile([P, QUAD, FEAT], F32, name="sums")
-            row_sum = sums[:, 0, 0:QUAD]
-            for s in range(PACK):
-                nc.tensor.matmul(
-                    out=row_sum, lhsT=fold[:, s, :], rhs=part_sb[:, s, :],
-                    start=(s == 0), stop=(s == PACK - 1),
-                )
-            deg = stream.tile([P, QUAD], F32, name="deg")
-            nc.vector.tensor_scalar(
-                out=deg[:], in0=row_sum, scalar1=1.0, scalar2=0.0, op0=ALU.add, op1=ALU.add
+        def row_sums(tile_no):
+            rows_sb = adj_of[tile_no]
+            copied = stream.tile([P, S_COLS], BF16, name="copied", bufs=1)
+            nc.scalar.activation(
+                out=copied[:], in_=rows_sb[:, 0:S_COLS], func=ACT.Copy,
+                accum_out=sum_s[:, tile_no : tile_no + 1],
             )
-            nc.gpsimd.tensor_tensor(out=dinv[:, tiles_of(quad)], in0=deg[:], in1=neg_half[:], op=ALU.pow)
+            pairs = stream.tile([P, V_HALF], F32, name="pairs", bufs=1)
+            nc.vector.scalar_tensor_tensor(
+                out=pairs[:], in0=rows_sb[:, S_COLS : S_COLS + V_HALF], scalar=1.0,
+                in1=rows_sb[:, S_COLS + V_HALF : NODES], op0=ALU.mult, op1=ALU.add,
+                accum_out=sum_v[:, tile_no : tile_no + 1],
+            )
+
+        def inverse_root_degrees(quad):
+            mine = tiles_of(quad)
+            row_sum = stream.tile([P, QUAD], F32, name="row_sum")
+            nc.gpsimd.tensor_tensor(out=row_sum[:], in0=sum_s[:, mine], in1=sum_v[:, mine], op=ALU.add)
+            deg = stream.tile([P, QUAD], F32, name="deg")
+            nc.gpsimd.tensor_scalar(
+                out=deg[:], in0=row_sum[:], scalar1=1.0, scalar2=1.0, op0=ALU.mult, op1=ALU.add
+            )
+            nc.gpsimd.tensor_tensor(out=dinv[:, mine], in0=deg[:], in1=neg_half[:], op=ALU.pow)
 
         def scale(quad):
             mine = tiles_of(quad)
@@ -217,76 +199,48 @@ def tile_gcnlayer_pa_t_kernel(tc, x, adj, W1_words, W1_scales, b1, ln_gamma, ln_
                 scales=hs_planes[:, quad, :],
                 in_=hs_grouped[:].rearrange("p f t -> p (f t)"),
             )
-            nc.gpsimd.tensor_tensor(
-                out=acc[:, mine, :],
-                in0=acc[:, mine, :],
-                in1=dinv[:, mine].unsqueeze(2).to_broadcast([P, QUAD, FEAT]),
-                op=ALU.mult,
-            )
+            for t in range(QUAD * quad, QUAD * (quad + 1)):
+                nc.vector.tensor_scalar(
+                    out=acc[:, t, :], in0=acc[:, t, :], scalar1=dinv[:, t : t + 1], scalar2=None,
+                    op0=ALU.mult,
+                )
 
-        def add_passes(quad, first, last):
+        for step in range(TILES):
+            quad, r = divmod(step, QUAD)
+            if r == 0:
+                x_quantised = flip_x(quad)
+            if step + AHEAD < TILES:
+                adj_of[step + AHEAD] = load_adj(step + AHEAD)
+            if r == 1 and quad + 1 < QUADS:
+                x_of[quad + 1] = load_x(quad + 1)
+            row_sums(step)
+            for k in range(0, PASSES, 2):
+                flip_adj(step, k)
+            if r == 0 and quad >= 1:
+                scale(quad - 1)
+            if r == 1:
+                if quad == 0:
+                    nc.vector.tensor_copy(out=rows[:], in_=rows_bf[:])
+                hidden(quad, x_quantised)
+            if r == QUAD - 1:
+                inverse_root_degrees(quad)
+        scale(QUADS - 1)
+
+        def aggregate(quad):
             sums = sum_psum.tile([P, QUAD, FEAT], F32, name="sums")
             for r in range(QUAD):
-                for g in range(first, last):
+                for g in range(PASSES):
                     nc.tensor.matmul_mx(
                         out=sums[:, r, :],
                         lhsT=codes[:, QUAD * quad + r, g, :].bitcast(FP8X4),
                         lhsT_scale=planes[4 * r : P, quad, g, :],
                         rhs=hs_codes[:, g, :].bitcast(FP8X4),
                         rhs_scale=hs_planes[:, g, :],
-                        start=(g == first),
-                        stop=(g == last - 1),
+                        start=(g == 0),
+                        stop=(g == PASSES - 1),
                     )
             mine = tiles_of(quad)
             nc.vector.tensor_tensor(out=acc[:, mine, :], in0=sums[:], in1=acc[:, mine, :], op=ALU.add)
-
-        def gets_early_passes(quad):
-            return EARLY <= quad < QUADS - 1
-
-        nc.vector.tensor_copy(out=rows[:], in_=rows_bf[:])
-        x_quantised = {}
-        for quad in range(X_AHEAD):
-            x_quantised[quad] = flip_x(quad)
-        for quad in range(X_AHEAD):
-            hidden(quad, x_quantised[quad])
-
-        grouped_of = {}
-        part_of = {}
-        part_sb_of = {}
-        for step in range(TILES + 3):
-            quad, r = divmod(step, QUAD)
-            done = quad - 1
-            soon = quad + X_AHEAD
-            if r == 0 and soon < QUADS:
-                x_of[soon] = load_x(soon)
-            if step + AHEAD < TILES:
-                adj_of[step + AHEAD] = load_adj(step + AHEAD)
-            if r == 2 and soon < QUADS:
-                x_quantised[soon] = flip_x(soon)
-            for s in range(PACK):
-                if 1 <= step <= TILES:
-                    before = step - 1
-                    if before % QUAD == 0 and s == 0:
-                        part_of[before // QUAD] = deg_psum.tile([P, QUAD, PACK, ONES], F32, name="part")
-                    row_sums(part_of[before // QUAD], before % QUAD, s, grouped_of[before])
-                if step < TILES:
-                    if s == 0:
-                        grouped_of[step] = []
-                    grouped_of[step].append(flip_adj(step, 2 * s))
-            if done >= 0 and r == 0:
-                part_sb_of[done] = gather(part_of[done])
-            if done >= 0 and r == 1:
-                degrees(done, part_sb_of[done])
-            if done >= 0 and r == 2:
-                scale(done)
-            if r == 3 and soon < QUADS:
-                hidden(soon, x_quantised[soon])
-            if r == 3 and gets_early_passes(done):
-                add_passes(done, 0, EARLY)
-
-        def aggregate(quad):
-            add_passes(quad, EARLY if gets_early_passes(quad) else 0, PASSES)
-            mine = tiles_of(quad)
             for t in range(QUAD * quad, QUAD * (quad + 1)):
                 nc.scalar.activation(
                     out=acc[:, t, :], in_=acc[:, t, :], func=ACT.Gelu,

@@ -11,6 +11,7 @@ I32 = mybir.dt.int32
 FP8X4 = mybir.dt.float8_e4m3fn_x4
 ACT = mybir.ActivationFunctionType
 ALU = mybir.AluOpType
+AXIS_X = mybir.AxisListType.X
 
 P = 128
 NODES = 4096
@@ -24,8 +25,10 @@ TILES = NODES // P
 QUAD = K_PASS // P
 QUADS = TILES // QUAD
 AHEAD = 3
-S_COLS = 1024
-V_HALF = (NODES - S_COLS) // 2
+X_AHEAD = 2
+EARLY = 2
+ONES = 14
+KEEP = 2
 
 FLOPS = 2 * NODES * K_IN * FEAT + 2 * NODES * NODES * FEAT
 
@@ -41,8 +44,10 @@ def tile_gcnlayer_pa_t_kernel(tc, x, adj, W1_words, W1_scales, b1, ln_gamma, ln_
         const = ctx.enter_context(tc.tile_pool(name="const", bufs=1))
         keep = ctx.enter_context(tc.tile_pool(name="keep", bufs=1))
         stream = ctx.enter_context(tc.tile_pool(name="stream", bufs=2))
-        flip_psum = ctx.enter_context(tc.psum_pool(name="flip_psum", bufs=6))
+        flip_psum = ctx.enter_context(tc.psum_pool(name="flip_psum", bufs=3))
+        idle_psum = ctx.enter_context(tc.psum_pool(name="idle_psum", bufs=1))
         sum_psum = ctx.enter_context(tc.psum_pool(name="sum_psum", bufs=2))
+        deg_psum = ctx.enter_context(tc.psum_pool(name="deg_psum", bufs=2))
         ctx.enter_context(tc.manual_schedule())
 
         def load_x(quad):
@@ -55,7 +60,9 @@ def tile_gcnlayer_pa_t_kernel(tc, x, adj, W1_words, W1_scales, b1, ln_gamma, ln_
             nc.sync.dma_start(out=adj_sb[:], in_=adj_view[tile_no // 2, tile_no % 2])
             return adj_sb
 
-        x_of = {0: load_x(0)}
+        x_of = {}
+        for quad in range(X_AHEAD):
+            x_of[quad] = load_x(quad)
         w1_codes = const.tile([P, FEAT], U32, align_bytes=64)
         nc.sync.dma_start(
             out=w1_codes[:].bitcast(I32),
@@ -81,8 +88,18 @@ def tile_gcnlayer_pa_t_kernel(tc, x, adj, W1_words, W1_scales, b1, ln_gamma, ln_
 
         ident = const.tile([P, P], F32)
         make_identity(nc, ident[:])
+        ones = const.tile([P, ONES], BF16)
+        nc.vector.memset(ones[:], 1.0)
         neg_half = const.tile([P, QUAD], F32)
         nc.vector.memset(neg_half[:], -0.5)
+        fold = const.tile([P, PACK, P], F32)
+        nc.vector.memset(fold[:], 0.0)
+        four_to_one = const.tile([P, P // PACK], F32)
+        nc.vector.tensor_reduce(
+            out=four_to_one[:], in_=ident[:].rearrange("p (i t) -> p i t", t=PACK), axis=AXIS_X, op=ALU.add
+        )
+        for s in range(PACK):
+            nc.vector.tensor_copy(out=fold[:, s, 32 * s : 32 * s + 32], in_=four_to_one[:])
         rows = const.tile([P, 3, FEAT], F32)
         b1_row, gamma_row, beta_row = rows[:, 0, :], rows[:, 1, :], rows[:, 2, :]
 
@@ -91,8 +108,6 @@ def tile_gcnlayer_pa_t_kernel(tc, x, adj, W1_words, W1_scales, b1, ln_gamma, ln_
         hs_codes = keep.tile([P, PASSES, FEAT], U32, align_bytes=64)
         hs_planes = keep.tile([P, PASSES, FEAT], U8, align_bytes=64)
         acc = keep.tile([P, TILES, FEAT], F32)
-        sum_s = keep.tile([P, TILES], F32)
-        sum_v = keep.tile([P, TILES], F32)
         dinv = keep.tile([P, TILES], F32)
         g_sum = keep.tile([P, TILES], F32)
         neg_mean = keep.tile([P, TILES], F32)
@@ -103,12 +118,27 @@ def tile_gcnlayer_pa_t_kernel(tc, x, adj, W1_words, W1_scales, b1, ln_gamma, ln_
         def tiles_of(quad):
             return slice(QUAD * quad, QUAD * (quad + 1))
 
+        unread = idle_psum.tile([P, KEEP, FEAT], F32)
+
+        def keep_clock_up():
+            for i in range(KEEP):
+                nc.tensor.matmul_mx(
+                    out=unread[:, i, :],
+                    lhsT=w1_codes[:].bitcast(FP8X4),
+                    lhsT_scale=w1_planes[:],
+                    rhs=w1_codes[:].bitcast(FP8X4),
+                    rhs_scale=w1_planes[:],
+                    start=True,
+                    stop=True,
+                )
+
         def flip_and_quantise(words, codes_out, planes_out):
+            keep_clock_up()
             bank = flip_psum.tile([P, 2, 2, P], F32, name="bank")
             for a in range(2):
                 for v in range(2):
                     nc.tensor.transpose(bank[:, a, v, :], words[a][v], ident[:])
-            grouped = stream.tile([P, 2, P, PACK], BF16, name="grouped", bufs=6, align_bytes=64)
+            grouped = stream.tile([P, 2, P, PACK], BF16, name="grouped", bufs=10, align_bytes=64)
             nc.scalar.copy(out=grouped[:].bitcast(F32), in_=bank[:].rearrange("p a v i -> p a i v"))
             nc.vector.quantize_mx(
                 out=codes_out.bitcast(FP8X4),
@@ -121,8 +151,8 @@ def tile_gcnlayer_pa_t_kernel(tc, x, adj, W1_words, W1_scales, b1, ln_gamma, ln_
             x_words = x_of[quad][:].bitcast(F32)
             quantised = []
             for u in range(2):
-                x_codes = stream.tile([P, 2, P], U32, name="x_codes", align_bytes=64)
-                x_planes = stream.tile([P, 2, P], U8, name="x_planes", align_bytes=64)
+                x_codes = stream.tile([P, 2, P], U32, name="x_codes", bufs=2 * X_AHEAD, align_bytes=64)
+                x_planes = stream.tile([P, 2, P], U8, name="x_planes", bufs=2 * X_AHEAD, align_bytes=64)
                 flip_and_quantise(
                     [[x_words[:, u, 256 * e + v : 256 * (e + 1) : 2] for v in range(2)] for e in range(2)],
                     x_codes[:].rearrange("p a i -> p (a i)"),
@@ -161,29 +191,34 @@ def tile_gcnlayer_pa_t_kernel(tc, x, adj, W1_words, W1_scales, b1, ln_gamma, ln_
                 planes[4 * (tile_no % QUAD) : P, tile_no // QUAD, k : k + 2, :].rearrange("p a i -> p (a i)"),
             )
 
-        def row_sums(tile_no):
-            rows_sb = adj_of[tile_no]
-            copied = stream.tile([P, S_COLS], BF16, name="copied", bufs=1)
-            nc.scalar.activation(
-                out=copied[:], in_=rows_sb[:, 0:S_COLS], func=ACT.Copy,
-                accum_out=sum_s[:, tile_no : tile_no + 1],
-            )
-            pairs = stream.tile([P, V_HALF], F32, name="pairs", bufs=1)
-            nc.vector.scalar_tensor_tensor(
-                out=pairs[:], in0=rows_sb[:, S_COLS : S_COLS + V_HALF], scalar=1.0,
-                in1=rows_sb[:, S_COLS + V_HALF : NODES], op0=ALU.mult, op1=ALU.add,
-                accum_out=sum_v[:, tile_no : tile_no + 1],
-            )
+        def row_sums(part, r, s, grouped):
+            for k in range(PASSES):
+                nc.tensor.matmul(
+                    out=part[:, r, s, :],
+                    lhsT=grouped[k // 2][:, k % 2, 32 * s : 32 * (s + 1), :].rearrange("p i t -> p (i t)"),
+                    rhs=ones[:],
+                    start=(k == 0),
+                    stop=(k == PASSES - 1),
+                )
 
-        def inverse_root_degrees(quad):
-            mine = tiles_of(quad)
-            row_sum = stream.tile([P, QUAD], F32, name="row_sum")
-            nc.gpsimd.tensor_tensor(out=row_sum[:], in0=sum_s[:, mine], in1=sum_v[:, mine], op=ALU.add)
+        def gather(part):
+            part_sb = stream.tile([P, PACK, QUAD], F32, name="part_sb")
+            nc.vector.tensor_copy(out=part_sb[:], in_=part[:, :, :, 0].rearrange("p r s -> p s r"))
+            return part_sb
+
+        def degrees(quad, part_sb):
+            sums = sum_psum.tile([P, QUAD, FEAT], F32, name="sums")
+            row_sum = sums[:, 0, 0:QUAD]
+            for s in range(PACK):
+                nc.tensor.matmul(
+                    out=row_sum, lhsT=fold[:, s, :], rhs=part_sb[:, s, :],
+                    start=(s == 0), stop=(s == PACK - 1),
+                )
             deg = stream.tile([P, QUAD], F32, name="deg")
-            nc.gpsimd.tensor_scalar(
-                out=deg[:], in0=row_sum[:], scalar1=1.0, scalar2=1.0, op0=ALU.mult, op1=ALU.add
+            nc.vector.tensor_scalar(
+                out=deg[:], in0=row_sum, scalar1=1.0, scalar2=0.0, op0=ALU.add, op1=ALU.add
             )
-            nc.gpsimd.tensor_tensor(out=dinv[:, mine], in0=deg[:], in1=neg_half[:], op=ALU.pow)
+            nc.gpsimd.tensor_tensor(out=dinv[:, tiles_of(quad)], in0=deg[:], in1=neg_half[:], op=ALU.pow)
 
         def scale(quad):
             mine = tiles_of(quad)
@@ -199,48 +234,78 @@ def tile_gcnlayer_pa_t_kernel(tc, x, adj, W1_words, W1_scales, b1, ln_gamma, ln_
                 scales=hs_planes[:, quad, :],
                 in_=hs_grouped[:].rearrange("p f t -> p (f t)"),
             )
-            for t in range(QUAD * quad, QUAD * (quad + 1)):
-                nc.vector.tensor_scalar(
-                    out=acc[:, t, :], in0=acc[:, t, :], scalar1=dinv[:, t : t + 1], scalar2=None,
-                    op0=ALU.mult,
-                )
+            nc.gpsimd.tensor_tensor(
+                out=acc[:, mine, :],
+                in0=acc[:, mine, :],
+                in1=dinv[:, mine].unsqueeze(2).to_broadcast([P, QUAD, FEAT]),
+                op=ALU.mult,
+            )
 
-        for step in range(TILES):
-            quad, r = divmod(step, QUAD)
-            if r == 0:
-                x_quantised = flip_x(quad)
-            if step + AHEAD < TILES:
-                adj_of[step + AHEAD] = load_adj(step + AHEAD)
-            if r == 1 and quad + 1 < QUADS:
-                x_of[quad + 1] = load_x(quad + 1)
-            row_sums(step)
-            for k in range(0, PASSES, 2):
-                flip_adj(step, k)
-            if r == 0 and quad >= 1:
-                scale(quad - 1)
-            if r == 1:
-                if quad == 0:
-                    nc.vector.tensor_copy(out=rows[:], in_=rows_bf[:])
-                hidden(quad, x_quantised)
-            if r == QUAD - 1:
-                inverse_root_degrees(quad)
-        scale(QUADS - 1)
-
-        def aggregate(quad):
+        def add_passes(quad, first, last):
             sums = sum_psum.tile([P, QUAD, FEAT], F32, name="sums")
             for r in range(QUAD):
-                for g in range(PASSES):
+                for g in range(first, last):
                     nc.tensor.matmul_mx(
                         out=sums[:, r, :],
                         lhsT=codes[:, QUAD * quad + r, g, :].bitcast(FP8X4),
                         lhsT_scale=planes[4 * r : P, quad, g, :],
                         rhs=hs_codes[:, g, :].bitcast(FP8X4),
                         rhs_scale=hs_planes[:, g, :],
-                        start=(g == 0),
-                        stop=(g == PASSES - 1),
+                        start=(g == first),
+                        stop=(g == last - 1),
                     )
             mine = tiles_of(quad)
             nc.vector.tensor_tensor(out=acc[:, mine, :], in0=sums[:], in1=acc[:, mine, :], op=ALU.add)
+
+        def gets_early_passes(quad):
+            return EARLY <= quad < QUADS - 1
+
+        nc.vector.tensor_copy(out=rows[:], in_=rows_bf[:])
+        for i in range(8):
+            keep_clock_up()
+        x_quantised = {}
+        for quad in range(X_AHEAD):
+            x_quantised[quad] = flip_x(quad)
+        for quad in range(X_AHEAD):
+            hidden(quad, x_quantised[quad])
+
+        grouped_of = {}
+        part_of = {}
+        part_sb_of = {}
+        for step in range(TILES + 3):
+            quad, r = divmod(step, QUAD)
+            done = quad - 1
+            soon = quad + X_AHEAD
+            if r == 0 and soon < QUADS:
+                x_of[soon] = load_x(soon)
+            if step + AHEAD < TILES:
+                adj_of[step + AHEAD] = load_adj(step + AHEAD)
+            if r == 2 and soon < QUADS:
+                x_quantised[soon] = flip_x(soon)
+            for s in range(PACK):
+                if 1 <= step <= TILES:
+                    before = step - 1
+                    if before % QUAD == 0 and s == 0:
+                        part_of[before // QUAD] = deg_psum.tile([P, QUAD, PACK, ONES], F32, name="part")
+                    row_sums(part_of[before // QUAD], before % QUAD, s, grouped_of[before])
+                if step < TILES:
+                    if s == 0:
+                        grouped_of[step] = []
+                    grouped_of[step].append(flip_adj(step, 2 * s))
+            if done >= 0 and r == 0:
+                part_sb_of[done] = gather(part_of[done])
+            if done >= 0 and r == 1:
+                degrees(done, part_sb_of[done])
+            if done >= 0 and r == 2:
+                scale(done)
+            if r == 3 and soon < QUADS:
+                hidden(soon, x_quantised[soon])
+            if r == 3 and gets_early_passes(done):
+                add_passes(done, 0, EARLY)
+
+        def aggregate(quad):
+            add_passes(quad, EARLY if gets_early_passes(quad) else 0, PASSES)
+            mine = tiles_of(quad)
             for t in range(QUAD * quad, QUAD * (quad + 1)):
                 nc.scalar.activation(
                     out=acc[:, t, :], in_=acc[:, t, :], func=ACT.Gelu,

@@ -11,7 +11,6 @@ I32 = mybir.dt.int32
 FP8X4 = mybir.dt.float8_e4m3fn_x4
 ACT = mybir.ActivationFunctionType
 ALU = mybir.AluOpType
-AXIS_X = mybir.AxisListType.X
 
 P = 128
 NODES = 4096
@@ -25,10 +24,9 @@ TILES = NODES // P
 QUAD = K_PASS // P
 QUADS = TILES // QUAD
 AHEAD = 3
-X_AHEAD = 2
-EARLY = 2
-ONES = 14
-KEEP = 2
+PE_PASSES = 2
+PE_COLS = PE_PASSES * K_PASS
+V_HALF = (NODES - PE_COLS) // 2
 
 FLOPS = 2 * NODES * K_IN * FEAT + 2 * NODES * NODES * FEAT
 
@@ -44,10 +42,9 @@ def tile_gcnlayer_pa_t_kernel(tc, x, adj, W1_words, W1_scales, b1, ln_gamma, ln_
         const = ctx.enter_context(tc.tile_pool(name="const", bufs=1))
         keep = ctx.enter_context(tc.tile_pool(name="keep", bufs=1))
         stream = ctx.enter_context(tc.tile_pool(name="stream", bufs=2))
-        flip_psum = ctx.enter_context(tc.psum_pool(name="flip_psum", bufs=3))
-        idle_psum = ctx.enter_context(tc.psum_pool(name="idle_psum", bufs=1))
+        flip_psum = ctx.enter_context(tc.psum_pool(name="flip_psum", bufs=5))
         sum_psum = ctx.enter_context(tc.psum_pool(name="sum_psum", bufs=2))
-        deg_psum = ctx.enter_context(tc.psum_pool(name="deg_psum", bufs=2))
+        deg_psum = ctx.enter_context(tc.psum_pool(name="deg_psum", bufs=1))
         ctx.enter_context(tc.manual_schedule())
 
         def load_x(quad):
@@ -60,9 +57,7 @@ def tile_gcnlayer_pa_t_kernel(tc, x, adj, W1_words, W1_scales, b1, ln_gamma, ln_
             nc.sync.dma_start(out=adj_sb[:], in_=adj_view[tile_no // 2, tile_no % 2])
             return adj_sb
 
-        x_of = {}
-        for quad in range(X_AHEAD):
-            x_of[quad] = load_x(quad)
+        x_of = {0: load_x(0)}
         w1_codes = const.tile([P, FEAT], U32, align_bytes=64)
         nc.sync.dma_start(
             out=w1_codes[:].bitcast(I32),
@@ -88,15 +83,16 @@ def tile_gcnlayer_pa_t_kernel(tc, x, adj, W1_words, W1_scales, b1, ln_gamma, ln_
 
         ident = const.tile([P, P], F32)
         make_identity(nc, ident[:])
-        ones = const.tile([P, ONES], BF16)
-        nc.vector.memset(ones[:], 1.0)
         neg_half = const.tile([P, QUAD], F32)
         nc.vector.memset(neg_half[:], -0.5)
+        ones = const.tile([P, 2], BF16)
+        nc.vector.memset(ones[:], 1.0)
         fold = const.tile([P, PACK, P], F32)
         nc.vector.memset(fold[:], 0.0)
         four_to_one = const.tile([P, P // PACK], F32)
         nc.vector.tensor_reduce(
-            out=four_to_one[:], in_=ident[:].rearrange("p (i t) -> p i t", t=PACK), axis=AXIS_X, op=ALU.add
+            out=four_to_one[:], in_=ident[:].rearrange("p (i t) -> p i t", t=PACK),
+            axis=mybir.AxisListType.X, op=ALU.add,
         )
         for s in range(PACK):
             nc.vector.tensor_copy(out=fold[:, s, 32 * s : 32 * s + 32], in_=four_to_one[:])
@@ -108,6 +104,7 @@ def tile_gcnlayer_pa_t_kernel(tc, x, adj, W1_words, W1_scales, b1, ln_gamma, ln_
         hs_codes = keep.tile([P, PASSES, FEAT], U32, align_bytes=64)
         hs_planes = keep.tile([P, PASSES, FEAT], U8, align_bytes=64)
         acc = keep.tile([P, TILES, FEAT], F32)
+        sum_v = keep.tile([P, TILES], F32)
         dinv = keep.tile([P, TILES], F32)
         g_sum = keep.tile([P, TILES], F32)
         neg_mean = keep.tile([P, TILES], F32)
@@ -118,28 +115,17 @@ def tile_gcnlayer_pa_t_kernel(tc, x, adj, W1_words, W1_scales, b1, ln_gamma, ln_
         def tiles_of(quad):
             return slice(QUAD * quad, QUAD * (quad + 1))
 
-        unread = idle_psum.tile([P, KEEP, FEAT], F32)
-
-        def keep_clock_up():
-            for i in range(KEEP):
-                nc.tensor.matmul_mx(
-                    out=unread[:, i, :],
-                    lhsT=w1_codes[:].bitcast(FP8X4),
-                    lhsT_scale=w1_planes[:],
-                    rhs=w1_codes[:].bitcast(FP8X4),
-                    rhs_scale=w1_planes[:],
-                    start=True,
-                    stop=True,
-                )
-
         def flip_and_quantise(words, codes_out, planes_out):
-            keep_clock_up()
-            bank = flip_psum.tile([P, 2, 2, P], F32, name="bank")
-            for a in range(2):
-                for v in range(2):
-                    nc.tensor.transpose(bank[:, a, v, :], words[a][v], ident[:])
-            grouped = stream.tile([P, 2, P, PACK], BF16, name="grouped", bufs=10, align_bytes=64)
-            nc.scalar.copy(out=grouped[:].bitcast(F32), in_=bank[:].rearrange("p a v i -> p a i v"))
+            grouped = stream.tile([P, 4, P, PACK], BF16, name="grouped", bufs=3, align_bytes=64)
+            for half in range(2):
+                bank = flip_psum.tile([P, 2, 2, P], F32, name="bank")
+                for a in range(2):
+                    for v in range(2):
+                        nc.tensor.transpose(bank[:, a, v, :], words[2 * half + a][v], ident[:])
+                nc.scalar.copy(
+                    out=grouped[:, 2 * half : 2 * half + 2, :, :].bitcast(F32),
+                    in_=bank[:].rearrange("p a v i -> p a i v"),
+                )
             nc.vector.quantize_mx(
                 out=codes_out.bitcast(FP8X4),
                 scales=planes_out,
@@ -149,32 +135,29 @@ def tile_gcnlayer_pa_t_kernel(tc, x, adj, W1_words, W1_scales, b1, ln_gamma, ln_
 
         def flip_x(quad):
             x_words = x_of[quad][:].bitcast(F32)
-            quantised = []
-            for u in range(2):
-                x_codes = stream.tile([P, 2, P], U32, name="x_codes", bufs=2 * X_AHEAD, align_bytes=64)
-                x_planes = stream.tile([P, 2, P], U8, name="x_planes", bufs=2 * X_AHEAD, align_bytes=64)
-                flip_and_quantise(
-                    [[x_words[:, u, 256 * e + v : 256 * (e + 1) : 2] for v in range(2)] for e in range(2)],
-                    x_codes[:].rearrange("p a i -> p (a i)"),
-                    x_planes[:].rearrange("p a i -> p (a i)"),
-                )
-                quantised.append((x_codes, x_planes))
-            return quantised
+            x_codes = stream.tile([P, QUAD, P], U32, name="x_codes", align_bytes=64)
+            x_planes = stream.tile([P, QUAD, P], U8, name="x_planes", align_bytes=64)
+            flip_and_quantise(
+                [[x_words[:, t // 2, 256 * (t % 2) + v : 256 * (t % 2 + 1) : 2] for v in range(2)]
+                 for t in range(QUAD)],
+                x_codes[:].rearrange("p a i -> p (a i)"),
+                x_planes[:].rearrange("p a i -> p (a i)"),
+            )
+            return x_codes, x_planes
 
         def hidden(quad, quantised):
+            x_codes, x_planes = quantised
             sums = sum_psum.tile([P, QUAD, FEAT], F32, name="sums")
-            for u in range(2):
-                x_codes, x_planes = quantised[u]
-                for e in range(2):
-                    nc.tensor.matmul_mx(
-                        out=sums[:, 2 * u + e, :],
-                        lhsT=x_codes[:, e, :].bitcast(FP8X4),
-                        lhsT_scale=x_planes[:, e, :],
-                        rhs=w1_codes[:].bitcast(FP8X4),
-                        rhs_scale=w1_planes[:],
-                        start=True,
-                        stop=True,
-                    )
+            for t in range(QUAD):
+                nc.tensor.matmul_mx(
+                    out=sums[:, t, :],
+                    lhsT=x_codes[:, t, :].bitcast(FP8X4),
+                    lhsT_scale=x_planes[:, t, :],
+                    rhs=w1_codes[:].bitcast(FP8X4),
+                    rhs_scale=w1_planes[:],
+                    start=True,
+                    stop=True,
+                )
             nc.vector.tensor_tensor(
                 out=acc[:, tiles_of(quad), :],
                 in0=sums[:],
@@ -186,39 +169,50 @@ def tile_gcnlayer_pa_t_kernel(tc, x, adj, W1_words, W1_scales, b1, ln_gamma, ln_
             adj_words = adj_of[tile_no][:].bitcast(F32)
             return flip_and_quantise(
                 [[adj_words[:, 256 * (k + a) + P * u : 256 * (k + a) + P * (u + 1)] for u in range(2)]
-                 for a in range(2)],
-                codes[:, tile_no, k : k + 2, :].rearrange("p a i -> p (a i)"),
-                planes[4 * (tile_no % QUAD) : P, tile_no // QUAD, k : k + 2, :].rearrange("p a i -> p (a i)"),
+                 for a in range(4)],
+                codes[:, tile_no, k : k + 4, :].rearrange("p a i -> p (a i)"),
+                planes[4 * (tile_no % QUAD) : P, tile_no // QUAD, k : k + 4, :].rearrange("p a i -> p (a i)"),
             )
 
-        def row_sums(part, r, s, grouped):
-            for k in range(PASSES):
-                nc.tensor.matmul(
-                    out=part[:, r, s, :],
-                    lhsT=grouped[k // 2][:, k % 2, 32 * s : 32 * (s + 1), :].rearrange("p i t -> p (i t)"),
-                    rhs=ones[:],
-                    start=(k == 0),
-                    stop=(k == PASSES - 1),
-                )
+        def row_sums_vector(tile_no):
+            rows_sb = adj_of[tile_no]
+            pairs = stream.tile([P, V_HALF], F32, name="pairs", bufs=1)
+            nc.vector.scalar_tensor_tensor(
+                out=pairs[:], in0=rows_sb[:, PE_COLS : PE_COLS + V_HALF], scalar=1.0,
+                in1=rows_sb[:, PE_COLS + V_HALF : NODES], op0=ALU.mult, op1=ALU.add,
+                accum_out=sum_v[:, tile_no : tile_no + 1],
+            )
+
+        def row_sums_tensor(part, r, grouped):
+            for s in range(PACK):
+                for k in range(PE_PASSES):
+                    nc.tensor.matmul(
+                        out=part[:, r, s, :],
+                        lhsT=grouped[:, k, 32 * s : 32 * (s + 1), :].rearrange("p i t -> p (i t)"),
+                        rhs=ones[:],
+                        start=(k == 0),
+                        stop=(k == PE_PASSES - 1),
+                    )
 
         def gather(part):
             part_sb = stream.tile([P, PACK, QUAD], F32, name="part_sb")
             nc.vector.tensor_copy(out=part_sb[:], in_=part[:, :, :, 0].rearrange("p r s -> p s r"))
             return part_sb
 
-        def degrees(quad, part_sb):
+        def inverse_root_degrees(quad, part_sb):
+            mine = tiles_of(quad)
             sums = sum_psum.tile([P, QUAD, FEAT], F32, name="sums")
-            row_sum = sums[:, 0, 0:QUAD]
+            first_cols = sums[:, 0, 0:QUAD]
             for s in range(PACK):
                 nc.tensor.matmul(
-                    out=row_sum, lhsT=fold[:, s, :], rhs=part_sb[:, s, :],
+                    out=first_cols, lhsT=fold[:, s, :], rhs=part_sb[:, s, :],
                     start=(s == 0), stop=(s == PACK - 1),
                 )
             deg = stream.tile([P, QUAD], F32, name="deg")
-            nc.vector.tensor_scalar(
-                out=deg[:], in0=row_sum, scalar1=1.0, scalar2=0.0, op0=ALU.add, op1=ALU.add
+            nc.vector.scalar_tensor_tensor(
+                out=deg[:], in0=first_cols, scalar=1.0, in1=sum_v[:, mine], op0=ALU.add, op1=ALU.add
             )
-            nc.gpsimd.tensor_tensor(out=dinv[:, tiles_of(quad)], in0=deg[:], in1=neg_half[:], op=ALU.pow)
+            nc.gpsimd.tensor_tensor(out=dinv[:, mine], in0=deg[:], in1=neg_half[:], op=ALU.pow)
 
         def scale(quad):
             mine = tiles_of(quad)
@@ -234,78 +228,51 @@ def tile_gcnlayer_pa_t_kernel(tc, x, adj, W1_words, W1_scales, b1, ln_gamma, ln_
                 scales=hs_planes[:, quad, :],
                 in_=hs_grouped[:].rearrange("p f t -> p (f t)"),
             )
-            nc.gpsimd.tensor_tensor(
-                out=acc[:, mine, :],
-                in0=acc[:, mine, :],
-                in1=dinv[:, mine].unsqueeze(2).to_broadcast([P, QUAD, FEAT]),
-                op=ALU.mult,
-            )
+            for t in range(QUAD * quad, QUAD * (quad + 1)):
+                nc.scalar.activation(
+                    out=acc[:, t, :], in_=acc[:, t, :], func=ACT.Copy, scale=dinv[:, t : t + 1]
+                )
 
-        def add_passes(quad, first, last):
+        for step in range(TILES + 2):
+            quad, r = divmod(step, QUAD)
+            if step < TILES:
+                if r == 0:
+                    x_quantised = flip_x(quad)
+                    part = deg_psum.tile([P, QUAD, PACK, 2], F32, name="part")
+                if step + AHEAD < TILES:
+                    adj_of[step + AHEAD] = load_adj(step + AHEAD)
+                if r == 1 and quad + 1 < QUADS:
+                    x_of[quad + 1] = load_x(quad + 1)
+                row_sums_vector(step)
+                first_passes = flip_adj(step, 0)
+                flip_adj(step, PASSES // 2)
+                row_sums_tensor(part, r, first_passes)
+                if r == QUAD - 1:
+                    part_sb = gather(part)
+                if r == 1:
+                    if quad == 0:
+                        nc.vector.tensor_copy(out=rows[:], in_=rows_bf[:])
+                    hidden(quad, x_quantised)
+            if quad >= 1 and r == 0:
+                inverse_root_degrees(quad - 1, part_sb)
+            if quad >= 1 and r == 1:
+                scale(quad - 1)
+
+        def aggregate(quad):
             sums = sum_psum.tile([P, QUAD, FEAT], F32, name="sums")
             for r in range(QUAD):
-                for g in range(first, last):
+                for g in range(PASSES):
                     nc.tensor.matmul_mx(
                         out=sums[:, r, :],
                         lhsT=codes[:, QUAD * quad + r, g, :].bitcast(FP8X4),
                         lhsT_scale=planes[4 * r : P, quad, g, :],
                         rhs=hs_codes[:, g, :].bitcast(FP8X4),
                         rhs_scale=hs_planes[:, g, :],
-                        start=(g == first),
-                        stop=(g == last - 1),
+                        start=(g == 0),
+                        stop=(g == PASSES - 1),
                     )
             mine = tiles_of(quad)
             nc.vector.tensor_tensor(out=acc[:, mine, :], in0=sums[:], in1=acc[:, mine, :], op=ALU.add)
-
-        def gets_early_passes(quad):
-            return EARLY <= quad < QUADS - 1
-
-        nc.vector.tensor_copy(out=rows[:], in_=rows_bf[:])
-        for i in range(8):
-            keep_clock_up()
-        x_quantised = {}
-        for quad in range(X_AHEAD):
-            x_quantised[quad] = flip_x(quad)
-        for quad in range(X_AHEAD):
-            hidden(quad, x_quantised[quad])
-
-        grouped_of = {}
-        part_of = {}
-        part_sb_of = {}
-        for step in range(TILES + 3):
-            quad, r = divmod(step, QUAD)
-            done = quad - 1
-            soon = quad + X_AHEAD
-            if r == 0 and soon < QUADS:
-                x_of[soon] = load_x(soon)
-            if step + AHEAD < TILES:
-                adj_of[step + AHEAD] = load_adj(step + AHEAD)
-            if r == 2 and soon < QUADS:
-                x_quantised[soon] = flip_x(soon)
-            for s in range(PACK):
-                if 1 <= step <= TILES:
-                    before = step - 1
-                    if before % QUAD == 0 and s == 0:
-                        part_of[before // QUAD] = deg_psum.tile([P, QUAD, PACK, ONES], F32, name="part")
-                    row_sums(part_of[before // QUAD], before % QUAD, s, grouped_of[before])
-                if step < TILES:
-                    if s == 0:
-                        grouped_of[step] = []
-                    grouped_of[step].append(flip_adj(step, 2 * s))
-            if done >= 0 and r == 0:
-                part_sb_of[done] = gather(part_of[done])
-            if done >= 0 and r == 1:
-                degrees(done, part_sb_of[done])
-            if done >= 0 and r == 2:
-                scale(done)
-            if r == 3 and soon < QUADS:
-                hidden(soon, x_quantised[soon])
-            if r == 3 and gets_early_passes(done):
-                add_passes(done, 0, EARLY)
-
-        def aggregate(quad):
-            add_passes(quad, EARLY if gets_early_passes(quad) else 0, PASSES)
-            mine = tiles_of(quad)
             for t in range(QUAD * quad, QUAD * (quad + 1)):
                 nc.scalar.activation(
                     out=acc[:, t, :], in_=acc[:, t, :], func=ACT.Gelu,

@@ -20,13 +20,15 @@ EPS = 1e-6
 PACK = 4
 K_PASS = P * PACK
 PASSES = NODES // K_PASS
+HALF_PASSES = PASSES // 2
 TILES = NODES // P
 QUAD = K_PASS // P
 QUADS = TILES // QUAD
 AHEAD = 3
-PE_PASSES = 2
-PE_COLS = PE_PASSES * K_PASS
-V_HALF = (NODES - PE_COLS) // 2
+S_COLS = 832
+V_HALF = (NODES - S_COLS) // 2
+BANKS = 7
+EARLY = 7
 
 FLOPS = 2 * NODES * K_IN * FEAT + 2 * NODES * NODES * FEAT
 
@@ -42,9 +44,8 @@ def tile_gcnlayer_pa_t_kernel(tc, x, adj, W1_words, W1_scales, b1, ln_gamma, ln_
         const = ctx.enter_context(tc.tile_pool(name="const", bufs=1))
         keep = ctx.enter_context(tc.tile_pool(name="keep", bufs=1))
         stream = ctx.enter_context(tc.tile_pool(name="stream", bufs=2))
-        flip_psum = ctx.enter_context(tc.psum_pool(name="flip_psum", bufs=5))
-        sum_psum = ctx.enter_context(tc.psum_pool(name="sum_psum", bufs=2))
-        deg_psum = ctx.enter_context(tc.psum_pool(name="deg_psum", bufs=1))
+        flip_psum = ctx.enter_context(tc.psum_pool(name="flip_psum", bufs=BANKS))
+        sum_psum = ctx.enter_context(tc.psum_pool(name="sum_psum", bufs=1))
         ctx.enter_context(tc.manual_schedule())
 
         def load_x(quad):
@@ -52,12 +53,15 @@ def tile_gcnlayer_pa_t_kernel(tc, x, adj, W1_words, W1_scales, b1, ln_gamma, ln_
             nc.sync.dma_start(out=x_sb[:], in_=x_view[quad])
             return x_sb
 
-        def load_adj(tile_no):
+        def load_adj(tile_no, parts=1):
             adj_sb = stream.tile([P, NODES], BF16, name="adj_sb", bufs=AHEAD + 1)
-            nc.sync.dma_start(out=adj_sb[:], in_=adj_view[tile_no // 2, tile_no % 2])
+            width = NODES // parts
+            for i in range(parts):
+                cols = slice(width * i, width * (i + 1))
+                nc.sync.dma_start(out=adj_sb[:, cols], in_=adj_view[tile_no // 2, tile_no % 2][:, cols])
             return adj_sb
 
-        x_of = {0: load_x(0)}
+        adj_of = {0: load_adj(0, 2)}
         w1_codes = const.tile([P, FEAT], U32, align_bytes=64)
         nc.sync.dma_start(
             out=w1_codes[:].bitcast(I32),
@@ -70,8 +74,8 @@ def tile_gcnlayer_pa_t_kernel(tc, x, adj, W1_words, W1_scales, b1, ln_gamma, ln_
                 out=w1_planes[32 * quadrant : 32 * quadrant + 4, :].bitcast(I32),
                 in_=W1_scales[0, 4 * quadrant : 4 * quadrant + 4, :].bitcast(I32),
             )
-        adj_of = {}
-        for tile_no in range(AHEAD):
+        x_of = {0: load_x(0)}
+        for tile_no in range(1, AHEAD):
             adj_of[tile_no] = load_adj(tile_no)
 
         rows_bf = const.tile([P, 3, FEAT], BF16)
@@ -85,17 +89,6 @@ def tile_gcnlayer_pa_t_kernel(tc, x, adj, W1_words, W1_scales, b1, ln_gamma, ln_
         make_identity(nc, ident[:])
         neg_half = const.tile([P, QUAD], F32)
         nc.vector.memset(neg_half[:], -0.5)
-        ones = const.tile([P, 2], BF16)
-        nc.vector.memset(ones[:], 1.0)
-        fold = const.tile([P, PACK, P], F32)
-        nc.vector.memset(fold[:], 0.0)
-        four_to_one = const.tile([P, P // PACK], F32)
-        nc.vector.tensor_reduce(
-            out=four_to_one[:], in_=ident[:].rearrange("p (i t) -> p i t", t=PACK),
-            axis=mybir.AxisListType.X, op=ALU.add,
-        )
-        for s in range(PACK):
-            nc.vector.tensor_copy(out=fold[:, s, 32 * s : 32 * s + 32], in_=four_to_one[:])
         rows = const.tile([P, 3, FEAT], F32)
         b1_row, gamma_row, beta_row = rows[:, 0, :], rows[:, 1, :], rows[:, 2, :]
 
@@ -105,6 +98,7 @@ def tile_gcnlayer_pa_t_kernel(tc, x, adj, W1_words, W1_scales, b1, ln_gamma, ln_
         hs_planes = keep.tile([P, PASSES, FEAT], U8, align_bytes=64)
         acc = keep.tile([P, TILES, FEAT], F32)
         sum_v = keep.tile([P, TILES], F32)
+        sum_s = keep.tile([P, TILES], F32)
         dinv = keep.tile([P, TILES], F32)
         g_sum = keep.tile([P, TILES], F32)
         neg_mean = keep.tile([P, TILES], F32)
@@ -115,8 +109,8 @@ def tile_gcnlayer_pa_t_kernel(tc, x, adj, W1_words, W1_scales, b1, ln_gamma, ln_
         def tiles_of(quad):
             return slice(QUAD * quad, QUAD * (quad + 1))
 
-        def flip_and_quantise(words, codes_out, planes_out):
-            grouped = stream.tile([P, 4, P, PACK], BF16, name="grouped", bufs=3, align_bytes=64)
+        def flip(words):
+            grouped = stream.tile([P, 4, P, PACK], BF16, name="grouped", bufs=4, align_bytes=64)
             for half in range(2):
                 bank = flip_psum.tile([P, 2, 2, P], F32, name="bank")
                 for a in range(2):
@@ -126,26 +120,43 @@ def tile_gcnlayer_pa_t_kernel(tc, x, adj, W1_words, W1_scales, b1, ln_gamma, ln_
                     out=grouped[:, 2 * half : 2 * half + 2, :, :].bitcast(F32),
                     in_=bank[:].rearrange("p a v i -> p a i v"),
                 )
+            return grouped
+
+        def quantise(grouped, codes_out, planes_out):
             nc.vector.quantize_mx(
-                out=codes_out.bitcast(FP8X4),
-                scales=planes_out,
+                out=codes_out.rearrange("p a i -> p (a i)").bitcast(FP8X4),
+                scales=planes_out.rearrange("p a i -> p (a i)"),
                 in_=grouped[:].rearrange("p a i t -> p (a i t)"),
             )
-            return grouped
 
         def flip_x(quad):
             x_words = x_of[quad][:].bitcast(F32)
+            return flip(
+                [[x_words[:, t // 2, 256 * (t % 2) + v : 256 * (t % 2 + 1) : 2] for v in range(2)]
+                 for t in range(QUAD)]
+            )
+
+        def quantise_x(grouped):
             x_codes = stream.tile([P, QUAD, P], U32, name="x_codes", align_bytes=64)
             x_planes = stream.tile([P, QUAD, P], U8, name="x_planes", align_bytes=64)
-            flip_and_quantise(
-                [[x_words[:, t // 2, 256 * (t % 2) + v : 256 * (t % 2 + 1) : 2] for v in range(2)]
-                 for t in range(QUAD)],
-                x_codes[:].rearrange("p a i -> p (a i)"),
-                x_planes[:].rearrange("p a i -> p (a i)"),
-            )
+            quantise(grouped, x_codes[:], x_planes[:])
             return x_codes, x_planes
 
-        def hidden(quad, quantised):
+        def flip_adj(tile_no, k):
+            adj_words = adj_of[tile_no][:].bitcast(F32)
+            return flip(
+                [[adj_words[:, 256 * (k + a) + P * u : 256 * (k + a) + P * (u + 1)] for u in range(2)]
+                 for a in range(4)]
+            )
+
+        def quantise_adj(tile_no, k, grouped):
+            quantise(
+                grouped,
+                codes[:, tile_no, k : k + 4, :],
+                planes[4 * (tile_no % QUAD) : P, tile_no // QUAD, k : k + 4, :],
+            )
+
+        def hidden_sums(quantised):
             x_codes, x_planes = quantised
             sums = sum_psum.tile([P, QUAD, FEAT], F32, name="sums")
             for t in range(QUAD):
@@ -158,6 +169,9 @@ def tile_gcnlayer_pa_t_kernel(tc, x, adj, W1_words, W1_scales, b1, ln_gamma, ln_
                     start=True,
                     stop=True,
                 )
+            return sums
+
+        def hidden(quad, sums):
             nc.vector.tensor_tensor(
                 out=acc[:, tiles_of(quad), :],
                 in0=sums[:],
@@ -165,52 +179,27 @@ def tile_gcnlayer_pa_t_kernel(tc, x, adj, W1_words, W1_scales, b1, ln_gamma, ln_
                 op=ALU.add,
             )
 
-        def flip_adj(tile_no, k):
-            adj_words = adj_of[tile_no][:].bitcast(F32)
-            return flip_and_quantise(
-                [[adj_words[:, 256 * (k + a) + P * u : 256 * (k + a) + P * (u + 1)] for u in range(2)]
-                 for a in range(4)],
-                codes[:, tile_no, k : k + 4, :].rearrange("p a i -> p (a i)"),
-                planes[4 * (tile_no % QUAD) : P, tile_no // QUAD, k : k + 4, :].rearrange("p a i -> p (a i)"),
+        def row_sums_scalar(tile_no):
+            copied = stream.tile([P, S_COLS], BF16, name="copied", bufs=1)
+            nc.scalar.activation(
+                out=copied[:], in_=adj_of[tile_no][:, 0:S_COLS], func=ACT.Copy,
+                accum_out=sum_s[:, tile_no : tile_no + 1],
             )
 
         def row_sums_vector(tile_no):
             rows_sb = adj_of[tile_no]
             pairs = stream.tile([P, V_HALF], F32, name="pairs", bufs=1)
             nc.vector.scalar_tensor_tensor(
-                out=pairs[:], in0=rows_sb[:, PE_COLS : PE_COLS + V_HALF], scalar=1.0,
-                in1=rows_sb[:, PE_COLS + V_HALF : NODES], op0=ALU.mult, op1=ALU.add,
+                out=pairs[:], in0=rows_sb[:, S_COLS : S_COLS + V_HALF], scalar=1.0,
+                in1=rows_sb[:, S_COLS + V_HALF : NODES], op0=ALU.mult, op1=ALU.add,
                 accum_out=sum_v[:, tile_no : tile_no + 1],
             )
 
-        def row_sums_tensor(part, r, grouped):
-            for s in range(PACK):
-                for k in range(PE_PASSES):
-                    nc.tensor.matmul(
-                        out=part[:, r, s, :],
-                        lhsT=grouped[:, k, 32 * s : 32 * (s + 1), :].rearrange("p i t -> p (i t)"),
-                        rhs=ones[:],
-                        start=(k == 0),
-                        stop=(k == PE_PASSES - 1),
-                    )
-
-        def gather(part):
-            part_sb = stream.tile([P, PACK, QUAD], F32, name="part_sb")
-            nc.vector.tensor_copy(out=part_sb[:], in_=part[:, :, :, 0].rearrange("p r s -> p s r"))
-            return part_sb
-
-        def inverse_root_degrees(quad, part_sb):
+        def inverse_root_degrees(quad):
             mine = tiles_of(quad)
-            sums = sum_psum.tile([P, QUAD, FEAT], F32, name="sums")
-            first_cols = sums[:, 0, 0:QUAD]
-            for s in range(PACK):
-                nc.tensor.matmul(
-                    out=first_cols, lhsT=fold[:, s, :], rhs=part_sb[:, s, :],
-                    start=(s == 0), stop=(s == PACK - 1),
-                )
             deg = stream.tile([P, QUAD], F32, name="deg")
             nc.vector.scalar_tensor_tensor(
-                out=deg[:], in0=first_cols, scalar=1.0, in1=sum_v[:, mine], op0=ALU.add, op1=ALU.add
+                out=deg[:], in0=sum_s[:, mine], scalar=1.0, in1=sum_v[:, mine], op0=ALU.add, op1=ALU.add
             )
             nc.gpsimd.tensor_tensor(out=dinv[:, mine], in0=deg[:], in1=neg_half[:], op=ALU.pow)
 
@@ -223,56 +212,77 @@ def tile_gcnlayer_pa_t_kernel(tc, x, adj, W1_words, W1_scales, b1, ln_gamma, ln_
                 in1=dinv[:, mine].unsqueeze(1).to_broadcast([P, FEAT, PACK]),
                 op=ALU.mult,
             )
+            return hs_grouped
+
+        def quantise_hs(quad, hs_grouped):
             nc.vector.quantize_mx(
                 out=hs_codes[:, quad, :].bitcast(FP8X4),
                 scales=hs_planes[:, quad, :],
                 in_=hs_grouped[:].rearrange("p f t -> p (f t)"),
             )
-            for t in range(QUAD * quad, QUAD * (quad + 1)):
-                nc.scalar.activation(
-                    out=acc[:, t, :], in_=acc[:, t, :], func=ACT.Copy, scale=dinv[:, t : t + 1]
+
+        for step in range(TILES):
+            quad, r = divmod(step, QUAD)
+            if step + AHEAD < TILES:
+                adj_of[step + AHEAD] = load_adj(step + AHEAD)
+            if r == 2 and quad + 1 < QUADS:
+                x_of[quad + 1] = load_x(quad + 1)
+            row_sums_scalar(step)
+            row_sums_vector(step)
+            first = flip_adj(step, 0)
+            if r == 2:
+                x_grouped = flip_x(quad)
+            second = flip_adj(step, HALF_PASSES)
+            if r == 0 and quad >= 1:
+                inverse_root_degrees(quad - 1)
+            if r == 2 and quad >= 1:
+                quantise_hs(quad - 1, hs_grouped)
+            quantise_adj(step, 0, first)
+            if r == 2:
+                x_quantised = quantise_x(x_grouped)
+            if r == 1 and quad >= 1:
+                hs_grouped = scale(quad - 1)
+            quantise_adj(step, HALF_PASSES, second)
+            if r == 3:
+                sums = hidden_sums(x_quantised)
+                if quad == 0:
+                    nc.vector.tensor_copy(out=rows[:], in_=rows_bf[:])
+                hidden(quad, sums)
+        inverse_root_degrees(QUADS - 1)
+        hs_grouped = scale(QUADS - 1)
+
+        def new_sums():
+            bank = flip_psum.tile([P, 2, 2, P], F32, name="bank")
+            return bank[:].rearrange("p a v f -> p (a v) f")
+
+        def add_passes(sums, quad, r, passes):
+            for g in passes:
+                nc.tensor.matmul_mx(
+                    out=sums[:, r, :],
+                    lhsT=codes[:, QUAD * quad + r, g, :].bitcast(FP8X4),
+                    lhsT_scale=planes[4 * r : P, quad, g, :],
+                    rhs=hs_codes[:, g, :].bitcast(FP8X4),
+                    rhs_scale=hs_planes[:, g, :],
+                    start=(g == 0),
+                    stop=(g == PASSES - 1),
                 )
 
-        for step in range(TILES + 2):
-            quad, r = divmod(step, QUAD)
-            if step < TILES:
-                if r == 0:
-                    x_quantised = flip_x(quad)
-                    part = deg_psum.tile([P, QUAD, PACK, 2], F32, name="part")
-                if step + AHEAD < TILES:
-                    adj_of[step + AHEAD] = load_adj(step + AHEAD)
-                if r == 1 and quad + 1 < QUADS:
-                    x_of[quad + 1] = load_x(quad + 1)
-                row_sums_vector(step)
-                first_passes = flip_adj(step, 0)
-                flip_adj(step, PASSES // 2)
-                row_sums_tensor(part, r, first_passes)
-                if r == QUAD - 1:
-                    part_sb = gather(part)
-                if r == 1:
-                    if quad == 0:
-                        nc.vector.tensor_copy(out=rows[:], in_=rows_bf[:])
-                    hidden(quad, x_quantised)
-            if quad >= 1 and r == 0:
-                inverse_root_degrees(quad - 1, part_sb)
-            if quad >= 1 and r == 1:
-                scale(quad - 1)
-
         def aggregate(quad):
-            sums = sum_psum.tile([P, QUAD, FEAT], F32, name="sums")
-            for r in range(QUAD):
-                for g in range(PASSES):
-                    nc.tensor.matmul_mx(
-                        out=sums[:, r, :],
-                        lhsT=codes[:, QUAD * quad + r, g, :].bitcast(FP8X4),
-                        lhsT_scale=planes[4 * r : P, quad, g, :],
-                        rhs=hs_codes[:, g, :].bitcast(FP8X4),
-                        rhs_scale=hs_planes[:, g, :],
-                        start=(g == 0),
-                        stop=(g == PASSES - 1),
-                    )
+            if quad < EARLY:
+                sums = early[quad]
+                add_passes(sums, quad, 0, (PASSES - 1,))
+            else:
+                sums = new_sums()
+                add_passes(sums, quad, 0, range(PASSES))
+            for r in range(1, QUAD):
+                add_passes(sums, quad, r, range(PASSES))
             mine = tiles_of(quad)
-            nc.vector.tensor_tensor(out=acc[:, mine, :], in0=sums[:], in1=acc[:, mine, :], op=ALU.add)
+            for r in range(QUAD):
+                t = QUAD * quad + r
+                nc.vector.scalar_tensor_tensor(
+                    out=acc[:, t, :], in0=acc[:, t, :], scalar=dinv[:, t : t + 1], in1=sums[:, r, :],
+                    op0=ALU.mult, op1=ALU.add,
+                )
             for t in range(QUAD * quad, QUAD * (quad + 1)):
                 nc.scalar.activation(
                     out=acc[:, t, :], in_=acc[:, t, :], func=ACT.Gelu,
@@ -303,6 +313,7 @@ def tile_gcnlayer_pa_t_kernel(tc, x, adj, W1_words, W1_scales, b1, ln_gamma, ln_
                     out=acc[:, t, :], in0=acc[:, t, :], scalar=neg_mean[:, t : t + 1], in1=gamma_row,
                     op0=ALU.add, op1=ALU.mult,
                 )
+            for t in range(QUAD * quad, QUAD * (quad + 1)):
                 nc.vector.scalar_tensor_tensor(
                     out=acc[:, t, :], in0=acc[:, t, :], scalar=rstd[:, t : t + 1], in1=beta_row,
                     op0=ALU.mult, op1=ALU.add,
@@ -311,6 +322,12 @@ def tile_gcnlayer_pa_t_kernel(tc, x, adj, W1_words, W1_scales, b1, ln_gamma, ln_
                 out=out_view[quad],
                 in_=acc[:, tiles_of(quad), :].rearrange("p (u e) f -> p u (e f)", u=2),
             )
+
+        early = []
+        for quad in range(EARLY):
+            early.append(new_sums())
+            add_passes(early[quad], quad, 0, range(PASSES - 1))
+        quantise_hs(QUADS - 1, hs_grouped)
 
         for quad in range(QUADS + 2):
             if quad < QUADS:

@@ -25,10 +25,11 @@ TILES = NODES // P
 QUAD = K_PASS // P
 QUADS = TILES // QUAD
 AHEAD = 3
-S_COLS = 832
+PE_TILES = (1,)
+S_COLS = 640
 V_HALF = (NODES - S_COLS) // 2
-BANKS = 7
-EARLY = 7
+BANKS = 6
+EARLY = 6
 
 FLOPS = 2 * NODES * K_IN * FEAT + 2 * NODES * NODES * FEAT
 
@@ -46,10 +47,11 @@ def tile_gcnlayer_pa_t_kernel(tc, x, adj, W1_words, W1_scales, b1, ln_gamma, ln_
         stream = ctx.enter_context(tc.tile_pool(name="stream", bufs=2))
         flip_psum = ctx.enter_context(tc.psum_pool(name="flip_psum", bufs=BANKS))
         sum_psum = ctx.enter_context(tc.psum_pool(name="sum_psum", bufs=1))
+        deg_psum = ctx.enter_context(tc.psum_pool(name="deg_psum", bufs=1))
         ctx.enter_context(tc.manual_schedule())
 
         def load_x(quad):
-            x_sb = stream.tile([P, 2, 2 * K_IN], BF16, name="x_sb")
+            x_sb = stream.tile([P, 2, 2 * K_IN], BF16, name="x_sb", bufs=1)
             nc.sync.dma_start(out=x_sb[:], in_=x_view[quad])
             return x_sb
 
@@ -89,6 +91,8 @@ def tile_gcnlayer_pa_t_kernel(tc, x, adj, W1_words, W1_scales, b1, ln_gamma, ln_
         make_identity(nc, ident[:])
         neg_half = const.tile([P, QUAD], F32)
         nc.vector.memset(neg_half[:], -0.5)
+        ones = const.tile([P, 2], BF16)
+        nc.vector.memset(ones[:], 1.0)
         rows = const.tile([P, 3, FEAT], F32)
         b1_row, gamma_row, beta_row = rows[:, 0, :], rows[:, 1, :], rows[:, 2, :]
 
@@ -99,6 +103,7 @@ def tile_gcnlayer_pa_t_kernel(tc, x, adj, W1_words, W1_scales, b1, ln_gamma, ln_
         acc = keep.tile([P, TILES, FEAT], F32)
         sum_v = keep.tile([P, TILES], F32)
         sum_s = keep.tile([P, TILES], F32)
+        nc.vector.memset(sum_v[:], 0.0)
         dinv = keep.tile([P, TILES], F32)
         g_sum = keep.tile([P, TILES], F32)
         neg_mean = keep.tile([P, TILES], F32)
@@ -110,7 +115,7 @@ def tile_gcnlayer_pa_t_kernel(tc, x, adj, W1_words, W1_scales, b1, ln_gamma, ln_
             return slice(QUAD * quad, QUAD * (quad + 1))
 
         def flip(words):
-            grouped = stream.tile([P, 4, P, PACK], BF16, name="grouped", bufs=4, align_bytes=64)
+            grouped = stream.tile([P, 4, P, PACK], BF16, name="grouped", bufs=5, align_bytes=64)
             for half in range(2):
                 bank = flip_psum.tile([P, 2, 2, P], F32, name="bank")
                 for a in range(2):
@@ -195,6 +200,20 @@ def tile_gcnlayer_pa_t_kernel(tc, x, adj, W1_words, W1_scales, b1, ln_gamma, ln_
                 accum_out=sum_v[:, tile_no : tile_no + 1],
             )
 
+        def row_sums_tensor(grouped):
+            sums = deg_psum.tile([P, 2], F32, name="row_sums")
+            for half in range(2):
+                for g in range(HALF_PASSES):
+                    for t in range(PACK):
+                        nc.tensor.matmul(
+                            out=sums[:],
+                            lhsT=grouped[half][:, g, :, t],
+                            rhs=ones[:],
+                            start=(half == 0 and g == 0 and t == 0),
+                            stop=(half == 1 and g == HALF_PASSES - 1 and t == PACK - 1),
+                        )
+            return sums
+
         def inverse_root_degrees(quad):
             mine = tiles_of(quad)
             deg = stream.tile([P, QUAD], F32, name="deg")
@@ -221,73 +240,76 @@ def tile_gcnlayer_pa_t_kernel(tc, x, adj, W1_words, W1_scales, b1, ln_gamma, ln_
                 in_=hs_grouped[:].rearrange("p f t -> p (f t)"),
             )
 
+        def on_tensor(tile_no):
+            return tile_no % QUAD in PE_TILES
+
+        def row_sums(tile_no):
+            if not on_tensor(tile_no):
+                row_sums_scalar(tile_no)
+                row_sums_vector(tile_no)
+
+        row_sums(0)
         for step in range(TILES):
             quad, r = divmod(step, QUAD)
             if step + AHEAD < TILES:
                 adj_of[step + AHEAD] = load_adj(step + AHEAD)
             if r == 2 and quad + 1 < QUADS:
                 x_of[quad + 1] = load_x(quad + 1)
-            row_sums_scalar(step)
-            row_sums_vector(step)
-            first = flip_adj(step, 0)
-            if r == 2:
+            halves = [flip_adj(step, 0), flip_adj(step, HALF_PASSES)]
+            if step > 0 and on_tensor(step - 1):
+                t_sums = row_sums_tensor(last_halves)
+            if r == 1:
                 x_grouped = flip_x(quad)
-            second = flip_adj(step, HALF_PASSES)
-            if r == 0 and quad >= 1:
-                inverse_root_degrees(quad - 1)
-            if r == 2 and quad >= 1:
-                quantise_hs(quad - 1, hs_grouped)
-            quantise_adj(step, 0, first)
-            if r == 2:
-                x_quantised = quantise_x(x_grouped)
-            if r == 1 and quad >= 1:
-                hs_grouped = scale(quad - 1)
-            quantise_adj(step, HALF_PASSES, second)
+            if step + 1 < TILES:
+                row_sums(step + 1)
+            quantise_adj(step, 0, halves[0])
             if r == 3:
+                inverse_root_degrees(quad)
+            quantise_adj(step, HALF_PASSES, halves[1])
+            if r == 1:
+                x_quantised = quantise_x(x_grouped)
+            if step > 0 and on_tensor(step - 1):
+                nc.vector.tensor_copy(out=sum_s[:, step - 1 : step], in_=t_sums[:, 0:1])
+            if r == 2:
                 sums = hidden_sums(x_quantised)
                 if quad == 0:
                     nc.vector.tensor_copy(out=rows[:], in_=rows_bf[:])
                 hidden(quad, sums)
-        inverse_root_degrees(QUADS - 1)
-        hs_grouped = scale(QUADS - 1)
+            if r == 0 and quad >= 1:
+                quantise_hs(quad - 1, hs_grouped)
+            if r == 3:
+                hs_grouped = scale(quad)
+            last_halves = halves
+        quantise_hs(QUADS - 1, hs_grouped)
 
         def new_sums():
             bank = flip_psum.tile([P, 2, 2, P], F32, name="bank")
-            return bank[:].rearrange("p a v f -> p (a v) f")
+            return bank[:, 0, 0, :]
 
-        def add_passes(sums, quad, r, passes):
+        def add_passes(sums, tile_no, passes):
+            r = tile_no % QUAD
             for g in passes:
                 nc.tensor.matmul_mx(
-                    out=sums[:, r, :],
-                    lhsT=codes[:, QUAD * quad + r, g, :].bitcast(FP8X4),
-                    lhsT_scale=planes[4 * r : P, quad, g, :],
+                    out=sums,
+                    lhsT=codes[:, tile_no, g, :].bitcast(FP8X4),
+                    lhsT_scale=planes[4 * r : P, tile_no // QUAD, g, :],
                     rhs=hs_codes[:, g, :].bitcast(FP8X4),
                     rhs_scale=hs_planes[:, g, :],
                     start=(g == 0),
                     stop=(g == PASSES - 1),
                 )
 
-        def aggregate(quad):
-            if quad < EARLY:
-                sums = early[quad]
-                add_passes(sums, quad, 0, (PASSES - 1,))
-            else:
-                sums = new_sums()
-                add_passes(sums, quad, 0, range(PASSES))
-            for r in range(1, QUAD):
-                add_passes(sums, quad, r, range(PASSES))
-            mine = tiles_of(quad)
-            for r in range(QUAD):
-                t = QUAD * quad + r
+        def gelus(quad, sums_of):
+            for t in range(QUAD * quad, QUAD * (quad + 1)):
                 nc.vector.scalar_tensor_tensor(
-                    out=acc[:, t, :], in0=acc[:, t, :], scalar=dinv[:, t : t + 1], in1=sums[:, r, :],
+                    out=acc[:, t, :], in0=acc[:, t, :], scalar=dinv[:, t : t + 1], in1=sums_of[t],
                     op0=ALU.mult, op1=ALU.add,
                 )
-            for t in range(QUAD * quad, QUAD * (quad + 1)):
                 nc.scalar.activation(
                     out=acc[:, t, :], in_=acc[:, t, :], func=ACT.Gelu,
                     scale=dinv[:, t : t + 1], accum_out=g_sum[:, t : t + 1],
                 )
+            mine = tiles_of(quad)
             nc.gpsimd.tensor_scalar(
                 out=neg_mean[:, mine], in0=g_sum[:, mine], scalar1=-1.0 / FEAT, scalar2=0.0,
                 op0=ALU.mult, op1=ALU.add,
@@ -323,15 +345,19 @@ def tile_gcnlayer_pa_t_kernel(tc, x, adj, W1_words, W1_scales, b1, ln_gamma, ln_
                 in_=acc[:, tiles_of(quad), :].rearrange("p (u e) f -> p u (e f)", u=2),
             )
 
-        early = []
-        for quad in range(EARLY):
-            early.append(new_sums())
-            add_passes(early[quad], quad, 0, range(PASSES - 1))
-        quantise_hs(QUADS - 1, hs_grouped)
-
+        sums_of = {}
+        for t in range(EARLY):
+            sums_of[t] = new_sums()
+            add_passes(sums_of[t], t, range(PASSES - 1))
+        for t in range(EARLY):
+            add_passes(sums_of[t], t, (PASSES - 1,))
         for quad in range(QUADS + 2):
             if quad < QUADS:
-                aggregate(quad)
+                for t in range(QUAD * quad, QUAD * (quad + 1)):
+                    if t >= EARLY:
+                        sums_of[t] = new_sums()
+                        add_passes(sums_of[t], t, range(PASSES))
+                gelus(quad, sums_of)
             if 1 <= quad <= QUADS:
                 spread(quad - 1)
             if quad >= 2:

@@ -25,9 +25,9 @@ TILES = NODES // P
 QUAD = K_PASS // P
 QUADS = TILES // QUAD
 AHEAD = 3
-PE_TILES = (1,)
-S_COLS = 640
+S_COLS = 512
 V_HALF = (NODES - S_COLS) // 2
+ONES = 36
 BANKS = 6
 EARLY = 6
 
@@ -64,6 +64,9 @@ def tile_gcnlayer_pa_t_kernel(tc, x, adj, W1_words, W1_scales, b1, ln_gamma, ln_
             return adj_sb
 
         adj_of = {0: load_adj(0, 2)}
+        adj_of[1] = load_adj(1)
+        x_of = {0: load_x(0)}
+        adj_of[2] = load_adj(2)
         w1_codes = const.tile([P, FEAT], U32, align_bytes=64)
         nc.sync.dma_start(
             out=w1_codes[:].bitcast(I32),
@@ -76,13 +79,9 @@ def tile_gcnlayer_pa_t_kernel(tc, x, adj, W1_words, W1_scales, b1, ln_gamma, ln_
                 out=w1_planes[32 * quadrant : 32 * quadrant + 4, :].bitcast(I32),
                 in_=W1_scales[0, 4 * quadrant : 4 * quadrant + 4, :].bitcast(I32),
             )
-        x_of = {0: load_x(0)}
-        for tile_no in range(1, AHEAD):
-            adj_of[tile_no] = load_adj(tile_no)
-
         rows_bf = const.tile([P, 3, FEAT], BF16)
         for i, vector in enumerate((b1, ln_gamma, ln_beta)):
-            nc.scalar.dma_start(out=rows_bf[:, i, :], in_=vector.partition_broadcast(P))
+            nc.sync.dma_start(out=rows_bf[:, i, :], in_=vector.partition_broadcast(P))
         warm = const.tile([P, 1], F32)
         nc.vector.memset(warm[:], 0.0)
         nc.scalar.activation(out=warm[:], in_=warm[:], func=ACT.Gelu)
@@ -91,7 +90,7 @@ def tile_gcnlayer_pa_t_kernel(tc, x, adj, W1_words, W1_scales, b1, ln_gamma, ln_
         make_identity(nc, ident[:])
         neg_half = const.tile([P, QUAD], F32)
         nc.vector.memset(neg_half[:], -0.5)
-        ones = const.tile([P, 2], BF16)
+        ones = const.tile([P, ONES], BF16)
         nc.vector.memset(ones[:], 1.0)
         rows = const.tile([P, 3, FEAT], F32)
         b1_row, gamma_row, beta_row = rows[:, 0, :], rows[:, 1, :], rows[:, 2, :]
@@ -201,7 +200,7 @@ def tile_gcnlayer_pa_t_kernel(tc, x, adj, W1_words, W1_scales, b1, ln_gamma, ln_
             )
 
         def row_sums_tensor(grouped):
-            sums = deg_psum.tile([P, 2], F32, name="row_sums")
+            sums = deg_psum.tile([P, ONES], F32, name="row_sums")
             for half in range(2):
                 for g in range(HALF_PASSES):
                     for t in range(PACK):
@@ -241,7 +240,8 @@ def tile_gcnlayer_pa_t_kernel(tc, x, adj, W1_words, W1_scales, b1, ln_gamma, ln_
             )
 
         def on_tensor(tile_no):
-            return tile_no % QUAD in PE_TILES
+            quad, r = divmod(tile_no, QUAD)
+            return r == 1 or (r == 0 and quad % 2 == 1)
 
         def row_sums(tile_no):
             if not on_tensor(tile_no):
@@ -264,7 +264,9 @@ def tile_gcnlayer_pa_t_kernel(tc, x, adj, W1_words, W1_scales, b1, ln_gamma, ln_
                 row_sums(step + 1)
             quantise_adj(step, 0, halves[0])
             if r == 3:
-                inverse_root_degrees(quad)
+                hs_grouped = scale(quad)
+                if step == TILES - 1:
+                    quantise_hs(quad, hs_grouped)
             quantise_adj(step, HALF_PASSES, halves[1])
             if r == 1:
                 x_quantised = quantise_x(x_grouped)
@@ -275,12 +277,11 @@ def tile_gcnlayer_pa_t_kernel(tc, x, adj, W1_words, W1_scales, b1, ln_gamma, ln_
                 if quad == 0:
                     nc.vector.tensor_copy(out=rows[:], in_=rows_bf[:])
                 hidden(quad, sums)
-            if r == 0 and quad >= 1:
-                quantise_hs(quad - 1, hs_grouped)
-            if r == 3:
-                hs_grouped = scale(quad)
+            if r == 2:
+                inverse_root_degrees(quad)
+            if r == 3 and step < TILES - 1:
+                quantise_hs(quad, hs_grouped)
             last_halves = halves
-        quantise_hs(QUADS - 1, hs_grouped)
 
         def new_sums():
             bank = flip_psum.tile([P, 2, 2, P], F32, name="bank")
@@ -299,50 +300,52 @@ def tile_gcnlayer_pa_t_kernel(tc, x, adj, W1_words, W1_scales, b1, ln_gamma, ln_
                     stop=(g == PASSES - 1),
                 )
 
-        def gelus(quad, sums_of):
-            for t in range(QUAD * quad, QUAD * (quad + 1)):
-                nc.vector.scalar_tensor_tensor(
-                    out=acc[:, t, :], in0=acc[:, t, :], scalar=dinv[:, t : t + 1], in1=sums_of[t],
-                    op0=ALU.mult, op1=ALU.add,
-                )
+        def gelu(t, sums):
+            nc.vector.scalar_tensor_tensor(
+                out=acc[:, t, :], in0=acc[:, t, :], scalar=dinv[:, t : t + 1], in1=sums,
+                op0=ALU.mult, op1=ALU.add,
+            )
+            nc.scalar.activation(
+                out=acc[:, t, :], in_=acc[:, t, :], func=ACT.Gelu,
+                scale=dinv[:, t : t + 1], accum_out=g_sum[:, t : t + 1],
+            )
+
+        def spread(mine):
+            for t in range(mine.start, mine.stop):
+                squares = stream.tile([P, FEAT], F32, name="squares")
                 nc.scalar.activation(
-                    out=acc[:, t, :], in_=acc[:, t, :], func=ACT.Gelu,
-                    scale=dinv[:, t : t + 1], accum_out=g_sum[:, t : t + 1],
+                    out=squares[:], in_=acc[:, t, :], func=ACT.Square, scale=-1.0 * FEAT,
+                    bias=g_sum[:, t : t + 1], accum_out=sq_sum[:, t : t + 1],
                 )
-            mine = tiles_of(quad)
+
+        def inverse_root_variance(mine):
+            nc.gpsimd.tensor_scalar(
+                out=var_eps[:, mine], in0=sq_sum[:, mine], scalar1=1.0 / (FEAT * FEAT * FEAT), scalar2=EPS,
+                op0=ALU.mult, op1=ALU.add,
+            )
+            nc.gpsimd.tensor_tensor(
+                out=rstd[:, mine], in0=var_eps[:, mine], in1=neg_half[:], op=ALU.pow
+            )
             nc.gpsimd.tensor_scalar(
                 out=neg_mean[:, mine], in0=g_sum[:, mine], scalar1=-1.0 / FEAT, scalar2=0.0,
                 op0=ALU.mult, op1=ALU.add,
             )
 
-        def spread(quad):
-            mine = tiles_of(quad)
-            for t in range(QUAD * quad, QUAD * (quad + 1)):
-                squares = stream.tile([P, FEAT], F32, name="squares")
-                nc.scalar.activation(
-                    out=squares[:], in_=acc[:, t, :], func=ACT.Square,
-                    bias=neg_mean[:, t : t + 1], accum_out=sq_sum[:, t : t + 1],
-                )
-            nc.gpsimd.tensor_scalar(
-                out=var_eps[:, mine], in0=sq_sum[:, mine], scalar1=1.0 / FEAT, scalar2=EPS,
-                op0=ALU.mult, op1=ALU.add,
-            )
-            nc.gpsimd.tensor_tensor(out=rstd[:, mine], in0=var_eps[:, mine], in1=neg_half[:], op=ALU.pow)
-
         def normalise_and_store(quad):
-            for t in range(QUAD * quad, QUAD * (quad + 1)):
+            mine = tiles_of(quad)
+            for t in range(mine.start, mine.stop):
                 nc.vector.scalar_tensor_tensor(
                     out=acc[:, t, :], in0=acc[:, t, :], scalar=neg_mean[:, t : t + 1], in1=gamma_row,
                     op0=ALU.add, op1=ALU.mult,
                 )
-            for t in range(QUAD * quad, QUAD * (quad + 1)):
+            for t in range(mine.start, mine.stop):
                 nc.vector.scalar_tensor_tensor(
                     out=acc[:, t, :], in0=acc[:, t, :], scalar=rstd[:, t : t + 1], in1=beta_row,
                     op0=ALU.mult, op1=ALU.add,
                 )
             nc.sync.dma_start(
                 out=out_view[quad],
-                in_=acc[:, tiles_of(quad), :].rearrange("p (u e) f -> p u (e f)", u=2),
+                in_=acc[:, mine, :].rearrange("p (u e) f -> p u (e f)", u=2),
             )
 
         sums_of = {}
@@ -351,14 +354,14 @@ def tile_gcnlayer_pa_t_kernel(tc, x, adj, W1_words, W1_scales, b1, ln_gamma, ln_
             add_passes(sums_of[t], t, range(PASSES - 1))
         for t in range(EARLY):
             add_passes(sums_of[t], t, (PASSES - 1,))
-        for quad in range(QUADS + 2):
-            if quad < QUADS:
-                for t in range(QUAD * quad, QUAD * (quad + 1)):
+        for i in range(QUADS + 2):
+            if i < QUADS:
+                for t in range(QUAD * i, QUAD * (i + 1)):
                     if t >= EARLY:
                         sums_of[t] = new_sums()
                         add_passes(sums_of[t], t, range(PASSES))
-                gelus(quad, sums_of)
-            if 1 <= quad <= QUADS:
-                spread(quad - 1)
-            if quad >= 2:
-                normalise_and_store(quad - 2)
+                    gelu(t, sums_of[t])
+                spread(tiles_of(i))
+                inverse_root_variance(tiles_of(i))
+            if i >= 2:
+                normalise_and_store(i - 2)

@@ -88,6 +88,8 @@ def tile_gcnlayer_pa_t_kernel(tc, x, adj, W1_words, W1_scales, b1, ln_gamma, ln_
 
         ident = const.tile([P, P], F32)
         make_identity(nc, ident[:])
+        eps = const.tile([P, 1], F32)
+        nc.vector.memset(eps[:], EPS)
         neg_half = const.tile([P, QUAD], F32)
         nc.vector.memset(neg_half[:], -0.5)
         ones = const.tile([P, ONES], BF16)
@@ -319,16 +321,15 @@ def tile_gcnlayer_pa_t_kernel(tc, x, adj, W1_words, W1_scales, b1, ln_gamma, ln_
                 )
 
         def inverse_root_variance(mine):
-            nc.gpsimd.tensor_scalar(
-                out=var_eps[:, mine], in0=sq_sum[:, mine], scalar1=1.0 / (FEAT * FEAT * FEAT), scalar2=EPS,
-                op0=ALU.mult, op1=ALU.add,
+            nc.scalar.activation(
+                out=neg_mean[:, mine], in_=g_sum[:, mine], func=ACT.Copy, scale=-1.0 / FEAT
+            )
+            nc.scalar.activation(
+                out=var_eps[:, mine], in_=sq_sum[:, mine], func=ACT.Identity,
+                scale=1.0 / (FEAT * FEAT * FEAT), bias=eps[:],
             )
             nc.gpsimd.tensor_tensor(
                 out=rstd[:, mine], in0=var_eps[:, mine], in1=neg_half[:], op=ALU.pow
-            )
-            nc.gpsimd.tensor_scalar(
-                out=neg_mean[:, mine], in0=g_sum[:, mine], scalar1=-1.0 / FEAT, scalar2=0.0,
-                op0=ALU.mult, op1=ALU.add,
             )
 
         def normalise_and_store(quad):

from contextlib import ExitStack

import concourse.mybir as mybir
from concourse.masks import make_identity

F32 = mybir.dt.float32
BF16 = mybir.dt.bfloat16
U32 = mybir.dt.uint32
U8 = mybir.dt.uint8
I32 = mybir.dt.int32
FP8X4 = mybir.dt.float8_e4m3fn_x4
ACT = mybir.ActivationFunctionType
ALU = mybir.AluOpType

P = 128
NODES = 4096
K_IN = 512
FEAT = 128
EPS = 1e-6
PACK = 4
K_PASS = P * PACK
PASSES = NODES // K_PASS
HALF_PASSES = PASSES // 2
TILES = NODES // P
QUAD = K_PASS // P
QUADS = TILES // QUAD
AHEAD = 3
S_COLS = 512
V_HALF = (NODES - S_COLS) // 2
ONES = 36
BANKS = 6
EARLY = 6

FLOPS = 2 * NODES * K_IN * FEAT + 2 * NODES * NODES * FEAT


def tile_gcnlayer_pa_t_kernel(tc, x, adj, W1_words, W1_scales, b1, ln_gamma, ln_beta, out):
    nc = tc.nc

    x_view = x.rearrange("(g u p e) k -> g p u (e k)", u=2, p=P, e=2)
    adj_view = adj.rearrange("(c p e) j -> c e p j", p=P, e=2)
    out_view = out.rearrange("(g u p e) f -> g p u (e f)", u=2, p=P, e=2)

    with ExitStack() as ctx:
        const = ctx.enter_context(tc.tile_pool(name="const", bufs=1))
        keep = ctx.enter_context(tc.tile_pool(name="keep", bufs=1))
        stream = ctx.enter_context(tc.tile_pool(name="stream", bufs=2))
        flip_psum = ctx.enter_context(tc.psum_pool(name="flip_psum", bufs=BANKS))
        sum_psum = ctx.enter_context(tc.psum_pool(name="sum_psum", bufs=1))
        deg_psum = ctx.enter_context(tc.psum_pool(name="deg_psum", bufs=1))
        ctx.enter_context(tc.manual_schedule())

        def load_x(quad):
            x_sb = stream.tile([P, 2, 2 * K_IN], BF16, name="x_sb", bufs=1)
            nc.sync.dma_start(out=x_sb[:], in_=x_view[quad])
            return x_sb

        def load_adj(tile_no, parts=1):
            adj_sb = stream.tile([P, NODES], BF16, name="adj_sb", bufs=AHEAD + 1)
            width = NODES // parts
            for i in range(parts):
                cols = slice(width * i, width * (i + 1))
                nc.sync.dma_start(out=adj_sb[:, cols], in_=adj_view[tile_no // 2, tile_no % 2][:, cols])
            return adj_sb

        adj_of = {0: load_adj(0, 2)}
        adj_of[1] = load_adj(1)
        x_of = {0: load_x(0)}
        adj_of[2] = load_adj(2)
        w1_codes = const.tile([P, FEAT], U32, align_bytes=64)
        nc.sync.dma_start(
            out=w1_codes[:].bitcast(I32),
            in_=W1_words[0].rearrange("p n t -> p (n t)").bitcast(I32),
        )
        w1_planes = const.tile([P, FEAT], U8, align_bytes=64)
        nc.vector.memset(w1_planes[:].bitcast(I32), 0)
        for quadrant in range(4):
            nc.sync.dma_start(
                out=w1_planes[32 * quadrant : 32 * quadrant + 4, :].bitcast(I32),
                in_=W1_scales[0, 4 * quadrant : 4 * quadrant + 4, :].bitcast(I32),
            )
        rows_bf = const.tile([P, 3, FEAT], BF16)
        for i, vector in enumerate((b1, ln_gamma, ln_beta)):
            nc.sync.dma_start(out=rows_bf[:, i, :], in_=vector.partition_broadcast(P))
        warm = const.tile([P, 1], F32)
        nc.vector.memset(warm[:], 0.0)
        nc.scalar.activation(out=warm[:], in_=warm[:], func=ACT.Gelu)

        ident = const.tile([P, P], F32)
        make_identity(nc, ident[:])
        eps = const.tile([P, 1], F32)
        nc.vector.memset(eps[:], EPS)
        neg_half = const.tile([P, QUAD], F32)
        nc.vector.memset(neg_half[:], -0.5)
        ones = const.tile([P, ONES], BF16)
        nc.vector.memset(ones[:], 1.0)
        rows = const.tile([P, 3, FEAT], F32)
        b1_row, gamma_row, beta_row = rows[:, 0, :], rows[:, 1, :], rows[:, 2, :]

        codes = keep.tile([P, TILES, PASSES, P], U32, align_bytes=64)
        planes = keep.tile([P, QUADS, PASSES, P], U8, align_bytes=64)
        hs_codes = keep.tile([P, PASSES, FEAT], U32, align_bytes=64)
        hs_planes = keep.tile([P, PASSES, FEAT], U8, align_bytes=64)
        acc = keep.tile([P, TILES, FEAT], F32)
        sum_v = keep.tile([P, TILES], F32)
        sum_s = keep.tile([P, TILES], F32)
        nc.vector.memset(sum_v[:], 0.0)
        dinv = keep.tile([P, TILES], F32)
        g_sum = keep.tile([P, TILES], F32)
        neg_mean = keep.tile([P, TILES], F32)
        sq_sum = keep.tile([P, TILES], F32)
        var_eps = keep.tile([P, TILES], F32)
        rstd = keep.tile([P, TILES], F32)

        def tiles_of(quad):
            return slice(QUAD * quad, QUAD * (quad + 1))

        def flip(words):
            grouped = stream.tile([P, 4, P, PACK], BF16, name="grouped", bufs=5, align_bytes=64)
            for half in range(2):
                bank = flip_psum.tile([P, 2, 2, P], F32, name="bank")
                for a in range(2):
                    for v in range(2):
                        nc.tensor.transpose(bank[:, a, v, :], words[2 * half + a][v], ident[:])
                nc.scalar.copy(
                    out=grouped[:, 2 * half : 2 * half + 2, :, :].bitcast(F32),
                    in_=bank[:].rearrange("p a v i -> p a i v"),
                )
            return grouped

        def quantise(grouped, codes_out, planes_out):
            nc.vector.quantize_mx(
                out=codes_out.rearrange("p a i -> p (a i)").bitcast(FP8X4),
                scales=planes_out.rearrange("p a i -> p (a i)"),
                in_=grouped[:].rearrange("p a i t -> p (a i t)"),
            )

        def flip_x(quad):
            x_words = x_of[quad][:].bitcast(F32)
            return flip(
                [[x_words[:, t // 2, 256 * (t % 2) + v : 256 * (t % 2 + 1) : 2] for v in range(2)]
                 for t in range(QUAD)]
            )

        def quantise_x(grouped):
            x_codes = stream.tile([P, QUAD, P], U32, name="x_codes", align_bytes=64)
            x_planes = stream.tile([P, QUAD, P], U8, name="x_planes", align_bytes=64)
            quantise(grouped, x_codes[:], x_planes[:])
            return x_codes, x_planes

        def flip_adj(tile_no, k):
            adj_words = adj_of[tile_no][:].bitcast(F32)
            return flip(
                [[adj_words[:, 256 * (k + a) + P * u : 256 * (k + a) + P * (u + 1)] for u in range(2)]
                 for a in range(4)]
            )

        def quantise_adj(tile_no, k, grouped):
            quantise(
                grouped,
                codes[:, tile_no, k : k + 4, :],
                planes[4 * (tile_no % QUAD) : P, tile_no // QUAD, k : k + 4, :],
            )

        def hidden_sums(quantised):
            x_codes, x_planes = quantised
            sums = sum_psum.tile([P, QUAD, FEAT], F32, name="sums")
            for t in range(QUAD):
                nc.tensor.matmul_mx(
                    out=sums[:, t, :],
                    lhsT=x_codes[:, t, :].bitcast(FP8X4),
                    lhsT_scale=x_planes[:, t, :],
                    rhs=w1_codes[:].bitcast(FP8X4),
                    rhs_scale=w1_planes[:],
                    start=True,
                    stop=True,
                )
            return sums

        def hidden(quad, sums):
            nc.vector.tensor_tensor(
                out=acc[:, tiles_of(quad), :],
                in0=sums[:],
                in1=b1_row.unsqueeze(1).to_broadcast([P, QUAD, FEAT]),
                op=ALU.add,
            )

        def row_sums_scalar(tile_no):
            copied = stream.tile([P, S_COLS], BF16, name="copied", bufs=1)
            nc.scalar.activation(
                out=copied[:], in_=adj_of[tile_no][:, 0:S_COLS], func=ACT.Copy,
                accum_out=sum_s[:, tile_no : tile_no + 1],
            )

        def row_sums_vector(tile_no):
            rows_sb = adj_of[tile_no]
            pairs = stream.tile([P, V_HALF], F32, name="pairs", bufs=1)
            nc.vector.scalar_tensor_tensor(
                out=pairs[:], in0=rows_sb[:, S_COLS : S_COLS + V_HALF], scalar=1.0,
                in1=rows_sb[:, S_COLS + V_HALF : NODES], op0=ALU.mult, op1=ALU.add,
                accum_out=sum_v[:, tile_no : tile_no + 1],
            )

        def row_sums_tensor(grouped):
            sums = deg_psum.tile([P, ONES], F32, name="row_sums")
            for half in range(2):
                for g in range(HALF_PASSES):
                    for t in range(PACK):
                        nc.tensor.matmul(
                            out=sums[:],
                            lhsT=grouped[half][:, g, :, t],
                            rhs=ones[:],
                            start=(half == 0 and g == 0 and t == 0),
                            stop=(half == 1 and g == HALF_PASSES - 1 and t == PACK - 1),
                        )
            return sums

        def inverse_root_degrees(quad):
            mine = tiles_of(quad)
            deg = stream.tile([P, QUAD], F32, name="deg")
            nc.vector.scalar_tensor_tensor(
                out=deg[:], in0=sum_s[:, mine], scalar=1.0, in1=sum_v[:, mine], op0=ALU.add, op1=ALU.add
            )
            nc.gpsimd.tensor_tensor(out=dinv[:, mine], in0=deg[:], in1=neg_half[:], op=ALU.pow)

        def scale(quad):
            mine = tiles_of(quad)
            hs_grouped = stream.tile([P, FEAT, PACK], BF16, name="hs_grouped", align_bytes=64)
            nc.vector.tensor_tensor(
                out=hs_grouped[:],
                in0=acc[:, mine, :].rearrange("p t f -> p f t"),
                in1=dinv[:, mine].unsqueeze(1).to_broadcast([P, FEAT, PACK]),
                op=ALU.mult,
            )
            return hs_grouped

        def quantise_hs(quad, hs_grouped):
            nc.vector.quantize_mx(
                out=hs_codes[:, quad, :].bitcast(FP8X4),
                scales=hs_planes[:, quad, :],
                in_=hs_grouped[:].rearrange("p f t -> p (f t)"),
            )

        def on_tensor(tile_no):
            quad, r = divmod(tile_no, QUAD)
            return r == 1 or (r == 0 and quad % 2 == 1)

        def row_sums(tile_no):
            if not on_tensor(tile_no):
                row_sums_scalar(tile_no)
                row_sums_vector(tile_no)

        row_sums(0)
        for step in range(TILES):
            quad, r = divmod(step, QUAD)
            if step + AHEAD < TILES:
                adj_of[step + AHEAD] = load_adj(step + AHEAD)
            if r == 2 and quad + 1 < QUADS:
                x_of[quad + 1] = load_x(quad + 1)
            halves = [flip_adj(step, 0), flip_adj(step, HALF_PASSES)]
            if step > 0 and on_tensor(step - 1):
                t_sums = row_sums_tensor(last_halves)
            if r == 1:
                x_grouped = flip_x(quad)
            if step + 1 < TILES:
                row_sums(step + 1)
            quantise_adj(step, 0, halves[0])
            if r == 3:
                hs_grouped = scale(quad)
                if step == TILES - 1:
                    quantise_hs(quad, hs_grouped)
            quantise_adj(step, HALF_PASSES, halves[1])
            if r == 1:
                x_quantised = quantise_x(x_grouped)
            if step > 0 and on_tensor(step - 1):
                nc.vector.tensor_copy(out=sum_s[:, step - 1 : step], in_=t_sums[:, 0:1])
            if r == 2:
                sums = hidden_sums(x_quantised)
                if quad == 0:
                    nc.vector.tensor_copy(out=rows[:], in_=rows_bf[:])
                hidden(quad, sums)
            if r == 2:
                inverse_root_degrees(quad)
            if r == 3 and step < TILES - 1:
                quantise_hs(quad, hs_grouped)
            last_halves = halves

        def new_sums():
            bank = flip_psum.tile([P, 2, 2, P], F32, name="bank")
            return bank[:, 0, 0, :]

        def add_passes(sums, tile_no, passes):
            r = tile_no % QUAD
            for g in passes:
                nc.tensor.matmul_mx(
                    out=sums,
                    lhsT=codes[:, tile_no, g, :].bitcast(FP8X4),
                    lhsT_scale=planes[4 * r : P, tile_no // QUAD, g, :],
                    rhs=hs_codes[:, g, :].bitcast(FP8X4),
                    rhs_scale=hs_planes[:, g, :],
                    start=(g == 0),
                    stop=(g == PASSES - 1),
                )

        def gelu(t, sums):
            nc.vector.scalar_tensor_tensor(
                out=acc[:, t, :], in0=acc[:, t, :], scalar=dinv[:, t : t + 1], in1=sums,
                op0=ALU.mult, op1=ALU.add,
            )
            nc.scalar.activation(
                out=acc[:, t, :], in_=acc[:, t, :], func=ACT.Gelu,
                scale=dinv[:, t : t + 1], accum_out=g_sum[:, t : t + 1],
            )

        def spread(mine):
            for t in range(mine.start, mine.stop):
                squares = stream.tile([P, FEAT], F32, name="squares")
                nc.scalar.activation(
                    out=squares[:], in_=acc[:, t, :], func=ACT.Square, scale=-1.0 * FEAT,
                    bias=g_sum[:, t : t + 1], accum_out=sq_sum[:, t : t + 1],
                )

        def inverse_root_variance(mine):
            nc.scalar.activation(
                out=neg_mean[:, mine], in_=g_sum[:, mine], func=ACT.Copy, scale=-1.0 / FEAT
            )
            nc.scalar.activation(
                out=var_eps[:, mine], in_=sq_sum[:, mine], func=ACT.Identity,
                scale=1.0 / (FEAT * FEAT * FEAT), bias=eps[:],
            )
            nc.gpsimd.tensor_tensor(
                out=rstd[:, mine], in0=var_eps[:, mine], in1=neg_half[:], op=ALU.pow
            )

        def normalise_and_store(quad):
            mine = tiles_of(quad)
            for t in range(mine.start, mine.stop):
                nc.vector.scalar_tensor_tensor(
                    out=acc[:, t, :], in0=acc[:, t, :], scalar=neg_mean[:, t : t + 1], in1=gamma_row,
                    op0=ALU.add, op1=ALU.mult,
                )
            for t in range(mine.start, mine.stop):
                nc.vector.scalar_tensor_tensor(
                    out=acc[:, t, :], in0=acc[:, t, :], scalar=rstd[:, t : t + 1], in1=beta_row,
                    op0=ALU.mult, op1=ALU.add,
                )
            nc.sync.dma_start(
                out=out_view[quad],
                in_=acc[:, mine, :].rearrange("p (u e) f -> p u (e f)", u=2),
            )

        sums_of = {}
        for t in range(EARLY):
            sums_of[t] = new_sums()
            add_passes(sums_of[t], t, range(PASSES - 1))
        for t in range(EARLY):
            add_passes(sums_of[t], t, (PASSES - 1,))
        for i in range(QUADS + 2):
            if i < QUADS:
                for t in range(QUAD * i, QUAD * (i + 1)):
                    if t >= EARLY:
                        sums_of[t] = new_sums()
                        add_passes(sums_of[t], t, range(PASSES))
                    gelu(t, sums_of[t])
                spread(tiles_of(i))
                inverse_root_variance(tiles_of(i))
            if i >= 2:
                normalise_and_store(i - 2)
